import numpy as np
import ml_dtypes


def mxq(x, axis, fmt="e4m3"):
    dtype, down = {"e4m3": (ml_dtypes.float8_e4m3fn, 7), "e5m2": (ml_dtypes.float8_e5m2, 14)}[fmt]
    v = np.moveaxis(np.asarray(x, np.float32).astype(ml_dtypes.bfloat16).astype(np.float64), axis, -1)
    blocks = v.reshape(v.shape[:-1] + (-1, 32))
    amax = np.abs(blocks).max(-1, keepdims=True)
    byte = np.maximum(np.where(amax > 0, np.frexp(amax)[1] - 1 + 127, 0) - down, 1)
    scale = np.exp2(byte - 127.0)
    codes = (blocks / scale).astype(np.float32).astype(dtype).astype(np.float64)
    return np.moveaxis((codes * scale).reshape(v.shape), -1, axis)


WIDE = False


def mx_kscale(k):
    if not WIDE:
        return np.ones(k)
    levels = np.array([10, -10, 5, -5, 0])
    if k % 512:
        return np.exp2(np.random.permutation(np.resize(levels, k // 32))).repeat(32)
    a = np.empty((k // 512, 16))
    for p in range(k // 512):
        a[p, :8] = np.random.permutation(np.resize(levels, 8))
        for g in range(8):
            far = levels[np.abs(levels - a[p, g]) >= 10]
            a[p, g + 8] = far[np.random.randint(len(far))]
    return np.exp2(a.ravel()).repeat(32)


BF16 = ml_dtypes.bfloat16


def bf(x):
    return np.asarray(x, np.float32).astype(BF16)


def f64(x):
    return np.asarray(x).astype(np.float64)


B, S, D, F, N = 2, 1024, 1024, 1024, 1024
SPARSITY = 0.1


def make_theta_sign(d1, d2, gain, row, col):
    mask = np.random.random((d1, d2)) < SPARSITY
    mag = np.abs(np.random.standard_normal((d1, d2))) * gain / np.sqrt(SPARSITY * d1)
    th = np.where(mask, mag, -mag) / row[:, None] * col
    sign = np.where(np.random.random((d1, d2)) < 0.5, -1.0, 1.0)
    return bf(th), bf(sign)


def draw0():
    s, t = mx_kscale(D), mx_kscale(F)
    x = bf(np.random.standard_normal((B, S, D)) * s)
    th1, sign1 = make_theta_sign(D, F, 1.0, s, t)
    th2, sign2 = make_theta_sign(F, N, 1.4, t, np.ones(N))
    return {"x": x, "th1": th1, "sign1": sign1, "th2": th2, "sign2": sign2, "relu": 1}


def core(x, th1, sign1, th2, sign2, relu):
    x = f64(x)
    for th, sign in ((f64(th1), f64(sign1)), (f64(th2), f64(sign2))):
        w = th * sign * (th > 0)
        x = mxq(x, 2, "e4m3") @ mxq(w, 0, "e4m3")
        if relu:
            x = np.maximum(x, 0.0)
    return x


def e4m3fn_bytes(y):
    return np.clip(np.asarray(y, np.float64), -448.0, 448.0).astype(np.float32).astype(ml_dtypes.float8_e4m3fn).view(np.uint8)


def e4m3fn_values(b):
    return np.asarray(b, np.uint8).view(ml_dtypes.float8_e4m3fn).astype(np.float64)


def setup_inputs():
    d = draw0()
    x0 = np.asarray(d['x']).astype(np.float64)
    s = (np.max(np.abs(x0), axis=(0, 1), keepdims=True) / 448.0).astype(np.float32)
    out = {}
    for k, v in d.items():
        if k == 'x':
            out['x_bytes'] = e4m3fn_bytes(x0 / s.astype(np.float64))
            out['x_scale'] = s
        else:
            out[k] = v
    return out


def reference(x_bytes, x_scale, th1, sign1, th2, sign2, relu):
    return core(e4m3fn_values(x_bytes) * x_scale.astype(np.float64), th1, sign1, th2, sign2, relu)

@@ -1,0 +1,245 @@
+from contextlib import ExitStack
+
+import concourse.mybir as mybir
+from concourse.masks import make_identity
+
+TOK, D, F, N = 2048, 1024, 1024, 1024
+FLOPS = 2 * TOK * D * F + 2 * TOK * F * N
+
+F32 = mybir.dt.float32
+BF16 = mybir.dt.bfloat16
+U32 = mybir.dt.uint32
+U8 = mybir.dt.uint8
+FP8 = mybir.dt.float8_e4m3fn
+FP8X4 = mybir.dt.float8_e4m3fn_x4
+ALU = mybir.AluOpType
+ACT = mybir.ActivationFunctionType
+P = 128
+HALF = 512
+
+
+def tile_sparse_connect_kernel(tc, x_bytes, x_scale, th1, sign1, th2, sign2, relu, out):
+    nc = tc.nc
+    x_rows = x_bytes.flatten_outer_dims()
+    out_rows = out.flatten_outer_dims()
+    raw = {
+        1: [a.rearrange("(g p j) f -> g p j f", p=P, j=4) for a in (th1, sign1)],
+        2: [a.rearrange("(g p j) f -> g p j f", p=P, j=4) for a in (th2, sign2)],
+    }
+    with ExitStack() as ctx:
+        keep = ctx.enter_context(tc.tile_pool(name="keep", bufs=1))
+        rawp = ctx.enter_context(tc.tile_pool(name="rawp", bufs=8))
+        grp = ctx.enter_context(tc.tile_pool(name="grp", bufs=3))
+        work = ctx.enter_context(tc.tile_pool(name="work", bufs=6))
+        deep = ctx.enter_context(tc.tile_pool(name="deep", bufs=8))
+        px = ctx.enter_context(tc.psum_pool(name="px", bufs=2))
+        ph = ctx.enter_context(tc.psum_pool(name="ph", bufs=3))
+        po = ctx.enter_context(tc.psum_pool(name="po", bufs=3))
+
+        ident = keep.tile([P, P], F32)
+        make_identity(nc, ident[:])
+        scale = keep.tile([P, D], F32)
+        th, sg, wp, wg, wq, ws = {}, {}, {}, {}, {}, {}
+        x8 = keep.tile([P, 16, D], U8, align_bytes=64)
+        xb, xt, xg, xq, xs, ht, hb, hq, hs, ot, ob = {}, {}, {}, {}, {}, {}, {}, {}, {}, {}, {}
+
+        def load_w(l, h, g):
+            cols = slice(h * HALF, (h + 1) * HALF)
+            t = rawp.tile([P, 4, HALF], BF16, name="th", align_bytes=64)
+            nc.sync.dma_start(out=t[:], in_=raw[l][0][g][:, :, cols])
+            s = rawp.tile([P, 4, HALF], BF16, name="sg", align_bytes=64)
+            nc.sync.dma_start(out=s[:], in_=raw[l][1][g][:, :, cols])
+            th[l, h, g], sg[l, h, g] = t, s
+
+        def load_scale():
+            nc.sync.dma_start(out=scale[:], in_=x_scale.rearrange("a b k -> (a b k)").partition_broadcast(P))
+
+        def load_x(i, n):
+            nc.sync.dma_start(
+                out=x8[:, i : i + n, :],
+                in_=x_rows[i * P : (i + n) * P, :].rearrange("(c p) d -> p c d", p=P),
+            )
+
+        def w_relu(l, h, g):
+            t = th[l, h, g]
+            nc.vector.tensor_scalar(out=t[:], in0=t[:], scalar1=0.0, scalar2=None, op0=ALU.max)
+
+        def w_prod(l, h, g):
+            t, s = th[l, h, g], sg[l, h, g]
+            nc.vector.tensor_tensor(out=t[:], in0=t[:], in1=s[:], op=ALU.mult)
+            wp[l, h, g] = t
+
+        def w_ilv(l, h, g):
+            w = grp.tile([P, 4 * HALF], BF16, name="w_grouped", align_bytes=64)
+            wg[l, h, g] = w
+            prod = wp[l, h, g]
+            if l == 1:
+                nc.scalar.copy(
+                    out=w[:].rearrange("p (t m j) -> p m t j", t=4, j=4),
+                    in_=prod[:].rearrange("p j (m t) -> p m t j", t=4),
+                )
+            else:
+                nc.scalar.copy(out=w[:].rearrange("p (n j) -> p n j", j=4), in_=prod[:].rearrange("p j n -> p n j"))
+
+        def w_stt(l, h, g):
+            t, s = th[l, h, g], sg[l, h, g]
+            w = grp.tile([P, 4 * HALF], BF16, name="w_grouped", align_bytes=64)
+            wg[l, h, g] = w
+            if l == 1:
+                for k in range(4):
+                    nc.vector.scalar_tensor_tensor(
+                        out=w[:].rearrange("p (t m j) -> p t m j", t=4, j=4)[:, k],
+                        in0=t[:].rearrange("p j (m t) -> p t m j", t=4)[:, k],
+                        scalar=0.0,
+                        in1=s[:].rearrange("p j (m t) -> p t m j", t=4)[:, k],
+                        op0=ALU.max,
+                        op1=ALU.mult,
+                    )
+            else:
+                nc.vector.scalar_tensor_tensor(
+                    out=w[:].rearrange("p (n j) -> p n j", j=4),
+                    in0=t[:].rearrange("p j n -> p n j"),
+                    scalar=0.0,
+                    in1=s[:].rearrange("p j n -> p n j"),
+                    op0=ALU.max,
+                    op1=ALU.mult,
+                )
+
+        def w_quant(l, h, g):
+            q = keep.tile([P, HALF], U32, name=f"wq{l}{h}{g}", align_bytes=64)
+            s = keep.tile([P, HALF], U8, name=f"ws{l}{h}{g}", align_bytes=64)
+            nc.vector.quantize_mx(out=q[:].bitcast(FP8X4), scales=s[:], in_=wg[l, h, g][:])
+            wq[l, h, g], ws[l, h, g] = q, s
+
+        def x_mul(i):
+            t = work.tile([P, D], BF16, name="xb", bufs=4, align_bytes=64)
+            nc.vector.tensor_tensor(out=t[:], in0=x8[:, i, :].bitcast(FP8), in1=scale[:], op=ALU.mult)
+            xb[i] = t
+
+        def x_tr(i):
+            t = px.tile([P, 2, 2, P], F32, name="xt")
+            words = xb[i][:].bitcast(F32)
+            for g in (0, 1):
+                for u in (0, 1):
+                    nc.tensor.transpose(t[:, g, u, :], words[:, 256 * g + u : 256 * (g + 1) : 2], ident[:])
+            xt[i] = t
+
+        def x_exit(i, eng):
+            i0, n = group[i]
+            if i0 not in xg:
+                xg[i0] = work.tile([P, n, 2, P, 2], F32, name="xg", bufs=3, align_bytes=64)
+            dst = xg[i0][:, i - i0]
+            src = xt[i][:].rearrange("p g u r -> p g r u")
+            if eng == "S":
+                nc.scalar.copy(out=dst, in_=src)
+            else:
+                nc.vector.tensor_copy(out=dst, in_=src)
+
+        def x_quant(i0):
+            n = group[i0][1]
+            q = deep.tile([P, n, 2, P], U32, name="xq", bufs=4, align_bytes=64)
+            s = deep.tile([P, n, 2, P], U8, name="xs", bufs=4, align_bytes=64)
+            nc.vector.quantize_mx(
+                out=q[:].rearrange("p c g r -> p (c g r)").bitcast(FP8X4),
+                scales=s[:].rearrange("p c g r -> p (c g r)"),
+                in_=xg[i0][:].rearrange("p c g r u -> p (c g r u)").bitcast(BF16),
+            )
+            for c in range(n):
+                xq[i0 + c], xs[i0 + c] = q[:, c], s[:, c]
+
+        def l1(i, h):
+            t = ph.tile([P, 4, P], F32, name="ht")
+            for k in range(4):
+                for g in (0, 1):
+                    nc.tensor.matmul_mx(
+                        out=t[:, k, :],
+                        lhsT=wq[1, h, g][:, k * P : (k + 1) * P].bitcast(FP8X4),
+                        lhsT_scale=ws[1, h, g][:, k * P : (k + 1) * P],
+                        rhs=xq[i][:, g].bitcast(FP8X4),
+                        rhs_scale=xs[i][:, g],
+                        start=(g == 0),
+                        stop=(g == 1),
+                    )
+            ht[i, h] = t
+
+        def h_exit(i, h, eng):
+            i0, n = group[i]
+            if i0 not in hb:
+                hb[i0] = work.tile([P, n, 2, P, 4], BF16, name="hb", bufs=4, align_bytes=64)
+            dst = hb[i0][:, i - i0, h]
+            src = ht[i, h][:].rearrange("p t n -> p n t")
+            if eng == "S":
+                nc.scalar.activation(out=dst, in_=src, func=ACT.Relu)
+            else:
+                nc.vector.tensor_scalar(out=dst, in0=src, scalar1=0.0, scalar2=None, op0=ALU.max)
+
+        def h_quant(i0):
+            n = group[i0][1]
+            q = deep.tile([P, n, 2, P], U32, name="hq", align_bytes=64)
+            s = deep.tile([P, n, 2, P], U8, name="hs", align_bytes=64)
+            nc.vector.quantize_mx(
+                out=q[:].rearrange("p c h r -> p (c h r)").bitcast(FP8X4),
+                scales=s[:].rearrange("p c h r -> p (c h r)"),
+                in_=hb[i0][:].rearrange("p c h r t -> p (c h r t)"),
+            )
+            for c in range(n):
+                hq[i0 + c], hs[i0 + c] = q[:, c], s[:, c]
+
+        def l2(i, n):
+            t = po.tile([P, HALF], F32, name="ot")
+            for h in (0, 1):
+                nc.tensor.matmul_mx(
+                    out=t[:],
+                    lhsT=hq[i][:, h].bitcast(FP8X4),
+                    lhsT_scale=hs[i][:, h],
+                    rhs=wq[2, n, h][:].bitcast(FP8X4),
+                    rhs_scale=ws[2, n, h][:],
+                    start=(h == 0),
+                    stop=(h == 1),
+                )
+            ot[i, n] = t
+
+        def o_exit(i, n, eng):
+            if i not in ob:
+                ob[i] = work.tile([P, N], F32, name="ob", bufs=12, align_bytes=64)
+            dst = ob[i][:, n * HALF : (n + 1) * HALF]
+            if eng == "S":
+                nc.scalar.activation(out=dst, in_=ot[i, n][:], func=ACT.Relu)
+            else:
+                nc.vector.tensor_scalar(out=dst, in0=ot[i, n][:], scalar1=0.0, scalar2=None, op0=ALU.max)
+
+        def store(i):
+            nc.sync.dma_start(out=out_rows[i * P : (i + 1) * P, :], in_=ob[i][:])
+        group = {}
+        for i0, n in [(0,2),(2,2),(4,2),(6,2),(8,2),(10,2),(12,2),(14,2)]:
+            for c in range(n):
+                group[i0 + c] = (i0, n)
+        run = {
+            "r": w_relu, "m": w_prod, "i": w_ilv, "t": w_stt, "q": w_quant,
+            "X": x_mul, "T": x_tr, "E": x_exit, "Q": x_quant,
+            "A": l1, "H": h_exit, "K": h_quant, "B": l2, "O": o_exit, "S": store, "w": load_w, "s": load_scale, "l": load_x,
+        }
+        order = (
+            "w,1,0,0 s l,0,2 w,1,0,1 l,2,2 w,1,1,0 w,1,1,1 l,4,4 w,2,0,0 w,2,0,1 w,2,1,0 w,2,1,1 l,8,8 "
+            "r,1,0,0 m,1,0,0 i,1,0,0 X,0 X,1 T,0 r,1,0,1 T,1 E,0,S q,1,0,0 E,1,S m,1,0,1 r,1,1,0 i,1,0,1 Q,0 "
+            "m,1,1,0 r,1,1,1 i,1,1,0 q,1,0,1 m,1,1,1 A,0,0 A,1,0 X,2 H,0,0,S H,1,0,S q,1,1,0 T,2 i,1,1,1 X,3 "
+            "X,4 T,3 X,5 E,2,S T,4 E,3,S q,1,1,1 T,5 E,4,S Q,2 A,0,1 E,5,S r,2,1,0 A,1,1 H,0,1,S Q,4 A,2,0 "
+            "H,1,1,S m,2,1,0 A,3,0 H,2,0,S A,4,0 H,3,0,S K,0 A,5,0 i,2,1,0 X,6 A,2,1 X,7 T,6 H,2,1,S X,8 T,7 "
+            "E,6,S A,3,1 q,2,1,0 E,7,S T,8 H,3,1,S X,9 A,4,1 E,8,S Q,6 H,4,0,S T,9 H,4,1,S K,2 A,5,1 E,9,S "
+            "X,10 A,6,0 H,5,0,S A,7,0 H,5,1,S Q,8 H,6,0,S A,6,1 t,2,1,1 H,7,0,S A,8,0 H,6,1,S A,9,0 H,8,0,S "
+            "A,7,1 K,4 H,9,0,S A,8,1 q,2,1,1 H,7,1,S T,10 X,11 H,8,1,S A,9,1 E,10,S B,0,1 K,6 H,9,1,S B,1,1 "
+            "t,2,0,0 O,0,1,S T,11 O,1,1,S B,2,1 B,3,1 E,11,S B,4,1 O,2,1,S K,8 B,5,1 O,3,1,S Q,10 B,6,1 "
+            "O,4,1,S q,2,0,0 B,7,1 O,5,1,S t,2,0,1 A,10,0 O,6,1,S A,11,0 O,7,1,S A,10,1 H,10,0,S H,11,0,S "
+            "A,11,1 X,12 H,10,1,S B,8,1 B,9,1 H,11,1,S q,2,0,1 T,12 O,8,1,S K,10 B,0,0 O,9,1,S X,13 B,1,0 "
+            "E,12,S B,2,0 O,0,0,S S,0 X,14 T,13 O,1,0,S S,1 B,3,0 O,2,0,S S,2 X,15 B,4,0 E,13,S T,14 O,3,0,S "
+            "S,3 Q,12 B,5,0 E,14,S O,4,0,V S,4 T,15 O,5,0,S S,5 A,12,0 E,15,V A,13,0 H,12,0,S Q,14 B,6,0 "
+            "H,13,0,S A,14,0 O,6,0,V S,6 A,15,0 H,14,0,S B,7,0 H,15,0,S A,12,1 O,7,0,V S,7 B,8,0 H,12,1,S "
+            "A,13,1 O,8,0,V S,8 B,9,0 H,13,1,S B,10,0 O,9,0,V S,9 B,10,1 O,10,0,S K,12 A,14,1 O,10,1,S S,10 "
+            "B,11,0 H,14,1,V B,11,1 O,11,0,S A,15,1 O,11,1,V S,11 B,12,0 H,15,1,S B,12,1 O,12,0,V B,13,0 "
+            "O,12,1,S S,12 K,14 B,13,1 O,13,0,S B,14,0 O,13,1,V S,13 B,14,1 O,14,0,S B,15,0 O,14,1,V S,14 "
+            "B,15,1 O,15,0,S O,15,1,V S,15 "
+        )
+        with tc.manual_schedule():
+            for token in order.split():
+                parts = token.split(",")
+                run[parts[0]](*[a if a in "SV" else int(a) for a in parts[1:]])

@@ -28,58 +28,86 @@ def tile_sparse_connect_kernel(tc, x_bytes, x_scale, th1, sign1, th2, sign2, rel
     }
     with ExitStack() as ctx:
         keep = ctx.enter_context(tc.tile_pool(name="keep", bufs=1))
-        rawp = ctx.enter_context(tc.tile_pool(name="rawp", bufs=8))
+        rawp = ctx.enter_context(tc.tile_pool(name="rawp", bufs=4))
         grp = ctx.enter_context(tc.tile_pool(name="grp", bufs=3))
         work = ctx.enter_context(tc.tile_pool(name="work", bufs=6))
-        deep = ctx.enter_context(tc.tile_pool(name="deep", bufs=8))
+        deep = ctx.enter_context(tc.tile_pool(name="deep", bufs=16))
         px = ctx.enter_context(tc.psum_pool(name="px", bufs=2))
         ph = ctx.enter_context(tc.psum_pool(name="ph", bufs=3))
         po = ctx.enter_context(tc.psum_pool(name="po", bufs=3))
 
         ident = keep.tile([P, P], F32)
         make_identity(nc, ident[:])
-        scale = keep.tile([P, D], F32)
-        th, sg, wp, wg, wq, ws = {}, {}, {}, {}, {}, {}
+        scale = keep.tile([P, D], F32, align_bytes=64)
+        s8 = keep.tile([P, 8], F32, align_bytes=64)
+        th, sg, wg, wq, ws = {}, {}, {}, {}, {}
         x8 = keep.tile([P, 16, D], U8, align_bytes=64)
         xb, xt, xg, xq, xs, ht, hb, hq, hs, ot, ob = {}, {}, {}, {}, {}, {}, {}, {}, {}, {}, {}
 
-        def load_w(l, h, g):
+        def load_w1(h, g):
             cols = slice(h * HALF, (h + 1) * HALF)
-            t = rawp.tile([P, 4, HALF], BF16, name="th", align_bytes=64)
-            nc.sync.dma_start(out=t[:], in_=raw[l][0][g][:, :, cols])
-            s = rawp.tile([P, 4, HALF], BF16, name="sg", align_bytes=64)
-            nc.sync.dma_start(out=s[:], in_=raw[l][1][g][:, :, cols])
-            th[l, h, g], sg[l, h, g] = t, s
+            t = rawp.tile([P, 4, HALF], BF16, name="th1_raw", align_bytes=64)
+            nc.sync.dma_start(out=t[:], in_=raw[1][0][g][:, :, cols])
+            s = rawp.tile([P, 4, HALF], BF16, name="sg1_raw", align_bytes=64)
+            nc.sync.dma_start(out=s[:], in_=raw[1][1][g][:, :, cols])
+            th[1, h, g], sg[1, h, g] = t[:], s[:]
+
+        def load_w2(g):
+            t = rawp.tile([P, 4, N], BF16, name="th2_raw", bufs=2, align_bytes=64)
+            nc.sync.dma_start(out=t[:], in_=raw[2][0][g])
+            s = rawp.tile([P, 4, N], BF16, name="sg2_raw", bufs=2, align_bytes=64)
+            nc.sync.dma_start(out=s[:], in_=raw[2][1][g])
+            for h in (0, 1):
+                cols = slice(h * HALF, (h + 1) * HALF)
+                th[2, h, g], sg[2, h, g] = t[:, :, cols], s[:, :, cols]
 
         def load_scale():
-            nc.sync.dma_start(out=scale[:], in_=x_scale.rearrange("a b k -> (a b k)").partition_broadcast(P))
+            nc.sync.dma_start(out=s8[:], in_=x_scale.rearrange("a b (p c) -> p (a b c)", c=8))
 
-        def load_x(i, n):
+        def spread_scale():
+            for b in (0, 1):
+                t = po.tile([P, HALF], F32, name="ot")
+                for c in range(4):
+                    k = 4 * b + c
+                    nc.tensor.matmul(
+                        out=t[:, c * P : (c + 1) * P],
+                        lhsT=s8[:, k : k + 1].to_broadcast([P, P]),
+                        rhs=ident[:],
+                        start=True,
+                        stop=True,
+                    )
+                nc.scalar.copy(
+                    out=scale[:].rearrange("p (q c) -> p q c", c=8)[:, :, 4 * b : 4 * b + 4],
+                    in_=t[:].rearrange("p (c q) -> p q c", c=4),
+                )
+
+        def load_x(b):
             nc.sync.dma_start(
-                out=x8[:, i : i + n, :],
-                in_=x_rows[i * P : (i + n) * P, :].rearrange("(c p) d -> p c d", p=P),
+                out=x8[:, 4 * b : 4 * b + 4, :],
+                in_=x_rows[4 * b * P : (4 * b + 4) * P, :].rearrange("(p c) d -> p c d", c=4),
             )
 
         def w_relu(l, h, g):
             t = th[l, h, g]
-            nc.vector.tensor_scalar(out=t[:], in0=t[:], scalar1=0.0, scalar2=None, op0=ALU.max)
+            nc.vector.tensor_scalar(out=t, in0=t, scalar1=0.0, scalar2=None, op0=ALU.max)
 
         def w_prod(l, h, g):
             t, s = th[l, h, g], sg[l, h, g]
-            nc.vector.tensor_tensor(out=t[:], in0=t[:], in1=s[:], op=ALU.mult)
-            wp[l, h, g] = t
+            nc.vector.tensor_tensor(out=t, in0=t, in1=s, op=ALU.mult)
 
-        def w_ilv(l, h, g):
+        def w_ilv(l, h, g, copy=nc.scalar.copy):
             w = grp.tile([P, 4 * HALF], BF16, name="w_grouped", align_bytes=64)
             wg[l, h, g] = w
-            prod = wp[l, h, g]
             if l == 1:
-                nc.scalar.copy(
+                copy(
                     out=w[:].rearrange("p (t m j) -> p m t j", t=4, j=4),
-                    in_=prod[:].rearrange("p j (m t) -> p m t j", t=4),
+                    in_=th[l, h, g].rearrange("p j (m t) -> p m t j", t=4),
                 )
             else:
-                nc.scalar.copy(out=w[:].rearrange("p (n j) -> p n j", j=4), in_=prod[:].rearrange("p j n -> p n j"))
+                copy(out=w[:].rearrange("p (n j) -> p n j", j=4), in_=th[l, h, g].rearrange("p j n -> p n j"))
+
+        def w_ilv_vector(l, h, g):
+            w_ilv(l, h, g, nc.vector.tensor_copy)
 
         def w_stt(l, h, g):
             t, s = th[l, h, g], sg[l, h, g]
@@ -89,18 +117,18 @@ def tile_sparse_connect_kernel(tc, x_bytes, x_scale, th1, sign1, th2, sign2, rel
                 for k in range(4):
                     nc.vector.scalar_tensor_tensor(
                         out=w[:].rearrange("p (t m j) -> p t m j", t=4, j=4)[:, k],
-                        in0=t[:].rearrange("p j (m t) -> p t m j", t=4)[:, k],
+                        in0=t.rearrange("p j (m t) -> p t m j", t=4)[:, k],
                         scalar=0.0,
-                        in1=s[:].rearrange("p j (m t) -> p t m j", t=4)[:, k],
+                        in1=s.rearrange("p j (m t) -> p t m j", t=4)[:, k],
                         op0=ALU.max,
                         op1=ALU.mult,
                     )
             else:
                 nc.vector.scalar_tensor_tensor(
                     out=w[:].rearrange("p (n j) -> p n j", j=4),
-                    in0=t[:].rearrange("p j n -> p n j"),
+                    in0=t.rearrange("p j n -> p n j"),
                     scalar=0.0,
-                    in1=s[:].rearrange("p j n -> p n j"),
+                    in1=s.rearrange("p j n -> p n j"),
                     op0=ALU.max,
                     op1=ALU.mult,
                 )
@@ -127,7 +155,7 @@ def tile_sparse_connect_kernel(tc, x_bytes, x_scale, th1, sign1, th2, sign2, rel
         def x_exit(i, eng):
             i0, n = group[i]
             if i0 not in xg:
-                xg[i0] = work.tile([P, n, 2, P, 2], F32, name="xg", bufs=3, align_bytes=64)
+                xg[i0] = work.tile([P, n, 2, P, 2], F32, name="xg", bufs=4, align_bytes=64)
             dst = xg[i0][:, i - i0]
             src = xt[i][:].rearrange("p g u r -> p g r u")
             if eng == "S":
@@ -209,35 +237,39 @@ def tile_sparse_connect_kernel(tc, x_bytes, x_scale, th1, sign1, th2, sign2, rel
                 nc.vector.tensor_scalar(out=dst, in0=ot[i, n][:], scalar1=0.0, scalar2=None, op0=ALU.max)
 
         def store(i):
-            nc.sync.dma_start(out=out_rows[i * P : (i + 1) * P, :], in_=ob[i][:])
+            b, c = divmod(i, 4)
+            dst = out_rows[4 * b * P : (4 * b + 4) * P, :].rearrange("(p c) n -> c p n", c=4)[c]
+            nc.sync.dma_start(out=dst, in_=ob[i][:])
         group = {}
-        for i0, n in [(0,2),(2,2),(4,2),(6,2),(8,2),(10,2),(12,2),(14,2)]:
+        for i0, n in [(0,1),(1,1),(2,1),(3,1),(4,1),(5,1),(6,1),(7,1),(8,1),(9,1),(10,1),(11,1),(12,1),(13,1),(14,1),(15,1)]:
             for c in range(n):
                 group[i0 + c] = (i0, n)
         run = {
             "r": w_relu, "m": w_prod, "i": w_ilv, "t": w_stt, "q": w_quant,
             "X": x_mul, "T": x_tr, "E": x_exit, "Q": x_quant,
-            "A": l1, "H": h_exit, "K": h_quant, "B": l2, "O": o_exit, "S": store, "w": load_w, "s": load_scale, "l": load_x,
+            "A": l1, "H": h_exit, "K": h_quant, "B": l2, "O": o_exit, "S": store, "w1": load_w1, "w2": load_w2,
+            "s": load_scale, "p": spread_scale, "l": load_x, "v": w_ilv_vector,
         }
         order = (
-            "w,1,0,0 s l,0,2 w,1,0,1 l,2,2 w,1,1,0 w,1,1,1 l,4,4 w,2,0,0 w,2,0,1 w,2,1,0 w,2,1,1 l,8,8 "
-            "r,1,0,0 m,1,0,0 i,1,0,0 X,0 X,1 T,0 r,1,0,1 T,1 E,0,S q,1,0,0 E,1,S m,1,0,1 r,1,1,0 i,1,0,1 Q,0 "
-            "m,1,1,0 r,1,1,1 i,1,1,0 q,1,0,1 m,1,1,1 A,0,0 A,1,0 X,2 H,0,0,S H,1,0,S q,1,1,0 T,2 i,1,1,1 X,3 "
-            "X,4 T,3 X,5 E,2,S T,4 E,3,S q,1,1,1 T,5 E,4,S Q,2 A,0,1 E,5,S r,2,1,0 A,1,1 H,0,1,S Q,4 A,2,0 "
-            "H,1,1,S m,2,1,0 A,3,0 H,2,0,S A,4,0 H,3,0,S K,0 A,5,0 i,2,1,0 X,6 A,2,1 X,7 T,6 H,2,1,S X,8 T,7 "
-            "E,6,S A,3,1 q,2,1,0 E,7,S T,8 H,3,1,S X,9 A,4,1 E,8,S Q,6 H,4,0,S T,9 H,4,1,S K,2 A,5,1 E,9,S "
-            "X,10 A,6,0 H,5,0,S A,7,0 H,5,1,S Q,8 H,6,0,S A,6,1 t,2,1,1 H,7,0,S A,8,0 H,6,1,S A,9,0 H,8,0,S "
-            "A,7,1 K,4 H,9,0,S A,8,1 q,2,1,1 H,7,1,S T,10 X,11 H,8,1,S A,9,1 E,10,S B,0,1 K,6 H,9,1,S B,1,1 "
-            "t,2,0,0 O,0,1,S T,11 O,1,1,S B,2,1 B,3,1 E,11,S B,4,1 O,2,1,S K,8 B,5,1 O,3,1,S Q,10 B,6,1 "
-            "O,4,1,S q,2,0,0 B,7,1 O,5,1,S t,2,0,1 A,10,0 O,6,1,S A,11,0 O,7,1,S A,10,1 H,10,0,S H,11,0,S "
-            "A,11,1 X,12 H,10,1,S B,8,1 B,9,1 H,11,1,S q,2,0,1 T,12 O,8,1,S K,10 B,0,0 O,9,1,S X,13 B,1,0 "
-            "E,12,S B,2,0 O,0,0,S S,0 X,14 T,13 O,1,0,S S,1 B,3,0 O,2,0,S S,2 X,15 B,4,0 E,13,S T,14 O,3,0,S "
-            "S,3 Q,12 B,5,0 E,14,S O,4,0,V S,4 T,15 O,5,0,S S,5 A,12,0 E,15,V A,13,0 H,12,0,S Q,14 B,6,0 "
-            "H,13,0,S A,14,0 O,6,0,V S,6 A,15,0 H,14,0,S B,7,0 H,15,0,S A,12,1 O,7,0,V S,7 B,8,0 H,12,1,S "
-            "A,13,1 O,8,0,V S,8 B,9,0 H,13,1,S B,10,0 O,9,0,V S,9 B,10,1 O,10,0,S K,12 A,14,1 O,10,1,S S,10 "
-            "B,11,0 H,14,1,V B,11,1 O,11,0,S A,15,1 O,11,1,V S,11 B,12,0 H,15,1,S B,12,1 O,12,0,V B,13,0 "
-            "O,12,1,S S,12 K,14 B,13,1 O,13,0,S B,14,0 O,13,1,V S,13 B,14,1 O,14,0,S B,15,0 O,14,1,V S,14 "
-            "B,15,1 O,15,0,S O,15,1,V S,15 "
+            "s w1,0,0 l,0 w1,0,1 w1,1,0 w1,1,1 l,1 w2,0 w2,1 l,2 l,3 p r,1,0,0 m,1,0,0 i,1,0,0 X,2 r,1,0,1 "
+            "T,2 X,1 E,2,S m,1,0,1 T,1 E,1,S r,1,1,0 i,1,0,1 Q,2 m,1,1,0 Q,1 r,1,1,1 q,1,0,0 i,1,1,0 q,1,0,1 "
+            "m,1,1,1 A,1,0 A,2,0 X,5 i,1,1,1 q,1,1,0 T,5 r,2,1,0 X,6 E,5,S X,4 T,6 H,1,0,S E,6,S q,1,1,1 T,4 "
+            "H,2,0,S m,2,1,0 A,1,1 E,4,S A,2,1 r,2,1,1 H,1,1,S Q,4 i,2,1,0 Q,6 A,4,1 K,1 Q,5 A,4,0 r,2,0,1 "
+            "m,2,1,1 H,2,1,S q,2,1,0 H,4,1,S A,5,0 H,4,0,V i,2,1,1 A,6,0 X,12 A,5,1 X,13 T,12 H,5,1,S K,4 "
+            "T,13 q,2,1,1 H,6,0,S A,6,1 X,14 E,12,S E,13,S B,4,1 Q,12 B,1,1 H,6,1,S Q,13 A,12,0 O,4,1,S K,2 "
+            "K,6 O,1,1,S A,12,1 X,15 H,12,0,S B,2,1 H,12,1,S A,13,1 H,5,0,V O,2,1,S T,15 m,2,0,1 H,13,1,S "
+            "T,14 E,15,S K,12 B,6,1 K,5 E,14,S X,10 B,12,1 i,2,0,1 B,5,1 Q,15 A,13,0 Q,14 X,9 A,15,0 A,14,1 "
+            "X,11 H,13,0,S T,10 H,14,1,S T,9 K,13 H,15,0,S q,2,0,1 A,14,0 O,5,1,S E,9,V A,15,1 O,6,1,S "
+            "E,10,V B,13,1 H,14,0,S Q,9 T,11 H,15,1,S Q,10 K,14 A,9,0 O,13,1,S r,2,0,0 E,11,S B,14,1 K,15 "
+            "m,2,0,0 H,9,0,S A,9,1 O,14,1,S B,15,1 Q,11 H,9,1,S A,10,1 X,0 i,2,0,0 A,11,0 K,9 A,11,1 X,3 "
+            "B,9,1 T,0 O,9,1,V H,10,1,S T,3 q,2,0,0 E,0,S A,10,0 H,11,1,V O,15,1,S B,12,0 Q,0 H,11,0,S "
+            "H,10,0,V B,15,0 E,3,S O,12,0,V A,0,0 O,15,0,S S,15 K,10 B,13,0 K,11 O,12,1,S S,12 Q,3 B,10,0 "
+            "X,8 H,0,0,S A,3,1 O,10,0,S B,9,0 O,13,0,V S,13 H,3,1,S B,4,0 X,7 O,9,0,S S,9 B,6,0 O,4,0,S S,4 "
+            "B,11,0 O,6,0,S S,6 B,1,0 O,11,0,S A,3,0 O,1,0,S S,1 B,11,1 H,3,0,S B,2,0 O,11,1,S S,11 B,14,0 "
+            "K,3 O,2,0,V S,2 B,10,1 O,14,0,S S,14 B,3,0 O,10,1,V S,10 B,3,1 O,3,0,S T,7 O,3,1,V S,3 T,8 "
+            "E,7,V B,5,0 E,8,S Q,7 A,0,1 O,5,0,V S,5 A,7,0 Q,8 H,0,1,V A,7,1 H,7,0,S A,8,0 K,0 H,7,1,S A,8,1 "
+            "H,8,0,S K,7 B,0,0 H,8,1,V B,0,1 O,0,0,V B,7,0 O,0,1,S S,0 K,8 B,7,1 O,7,0,V B,8,1 O,7,1,S S,7 "
+            "B,8,0 O,8,1,S O,8,0,S S,8 "
         )
         with tc.manual_schedule():
             for token in order.split():

@@ -41,15 +41,20 @@ def tile_sparse_connect_kernel(tc, x_bytes, x_scale, th1, sign1, th2, sign2, rel
         scale = keep.tile([P, D], F32, align_bytes=64)
         s8 = keep.tile([P, 8], F32, align_bytes=64)
         th, sg, wg, wq, ws = {}, {}, {}, {}, {}
+        block = {}
         x8 = keep.tile([P, 16, D], U8, align_bytes=64)
         xb, xt, xg, xq, xs, ht, hb, hq, hs, ot, ob = {}, {}, {}, {}, {}, {}, {}, {}, {}, {}, {}
+
+        def parts(l, h, g):
+            return (slice(0, 2), slice(2, 4)) if (l, h, g) == (1, 0, 0) else (slice(0, 4),)
 
         def load_w1(h, g):
             cols = slice(h * HALF, (h + 1) * HALF)
             t = rawp.tile([P, 4, HALF], BF16, name="th1_raw", align_bytes=64)
-            nc.sync.dma_start(out=t[:], in_=raw[1][0][g][:, :, cols])
             s = rawp.tile([P, 4, HALF], BF16, name="sg1_raw", align_bytes=64)
-            nc.sync.dma_start(out=s[:], in_=raw[1][1][g][:, :, cols])
+            for dst, src in ((t, raw[1][0][g]), (s, raw[1][1][g])):
+                for rows in parts(1, h, g):
+                    nc.sync.dma_start(out=dst[:, rows], in_=src[:, rows, cols])
             th[1, h, g], sg[1, h, g] = t[:], s[:]
 
         def load_w2(g):
@@ -62,7 +67,7 @@ def tile_sparse_connect_kernel(tc, x_bytes, x_scale, th1, sign1, th2, sign2, rel
                 th[2, h, g], sg[2, h, g] = t[:, :, cols], s[:, :, cols]
 
         def load_scale():
-            nc.sync.dma_start(out=s8[:], in_=x_scale.rearrange("a b (p c) -> p (a b c)", c=8))
+            nc.scalar.dma_start(out=s8[:], in_=x_scale.rearrange("a b (p c) -> p (a b c)", c=8))
 
         def spread_scale():
             for b in (0, 1):
@@ -81,33 +86,56 @@ def tile_sparse_connect_kernel(tc, x_bytes, x_scale, th1, sign1, th2, sign2, rel
                     in_=t[:].rearrange("p (c q) -> p q c", c=4),
                 )
 
-        def load_x(b):
+        def load_x(i, n):
+            block[i] = (i, n)
             nc.sync.dma_start(
-                out=x8[:, 4 * b : 4 * b + 4, :],
-                in_=x_rows[4 * b * P : (4 * b + 4) * P, :].rearrange("(p c) d -> p c d", c=4),
+                out=x8[:, i : i + n, :],
+                in_=x_rows[i * P : (i + n) * P, :].rearrange("(p c) d -> p c d", c=n),
             )
+
+        def warm(n):
+            t = po.tile([P, HALF], F32, name="ot")
+            for c in range(n):
+                nc.tensor.matmul(out=t[:, c * P : (c + 1) * P], lhsT=ident[:], rhs=ident[:], start=True, stop=True)
 
         def w_relu(l, h, g):
             t = th[l, h, g]
-            nc.vector.tensor_scalar(out=t, in0=t, scalar1=0.0, scalar2=None, op0=ALU.max)
+            for rows in parts(l, h, g):
+                nc.vector.tensor_scalar(out=t[:, rows], in0=t[:, rows], scalar1=0.0, scalar2=None, op0=ALU.max)
 
         def w_prod(l, h, g):
             t, s = th[l, h, g], sg[l, h, g]
-            nc.vector.tensor_tensor(out=t, in0=t, in1=s, op=ALU.mult)
+            for rows in parts(l, h, g):
+                nc.vector.tensor_tensor(out=t[:, rows], in0=t[:, rows], in1=s[:, rows], op=ALU.mult)
 
-        def w_ilv(l, h, g, copy=nc.scalar.copy):
-            w = grp.tile([P, 4 * HALF], BF16, name="w_grouped", align_bytes=64)
-            wg[l, h, g] = w
+        def w_ilv_part(l, h, g, copy, part):
+            if (l, h, g) not in wg:
+                wg[l, h, g] = grp.tile([P, 4 * HALF], BF16, name="w_grouped", align_bytes=64)
+            w = wg[l, h, g]
             if l == 1:
+                sel = slice(4 * part.start // HALF, 4 * part.stop // HALF)
                 copy(
-                    out=w[:].rearrange("p (t m j) -> p m t j", t=4, j=4),
-                    in_=th[l, h, g].rearrange("p j (m t) -> p m t j", t=4),
+                    out=w[:].rearrange("p (t m j) -> p m t j", t=4, j=4)[:, :, sel],
+                    in_=th[l, h, g].rearrange("p j (m t) -> p m t j", t=4)[:, :, sel],
                 )
             else:
-                copy(out=w[:].rearrange("p (n j) -> p n j", j=4), in_=th[l, h, g].rearrange("p j n -> p n j"))
+                cols = slice(part.start // 4, part.stop // 4)
+                copy(
+                    out=w[:].rearrange("p (c i j) -> p c j i", i=4, j=4)[:, cols],
+                    in_=th[l, h, g].rearrange("p j (c i) -> p c j i", i=4)[:, cols],
+                )
+
+        def w_ilv(l, h, g):
+            w_ilv_part(l, h, g, nc.scalar.copy, slice(0, HALF))
 
         def w_ilv_vector(l, h, g):
-            w_ilv(l, h, g, nc.vector.tensor_copy)
+            w_ilv_part(l, h, g, nc.vector.tensor_copy, slice(0, HALF))
+
+        def w_ilv_left(l, h, g):
+            w_ilv_part(l, h, g, nc.scalar.copy, slice(0, HALF // 2))
+
+        def w_ilv_right(l, h, g):
+            w_ilv_part(l, h, g, nc.vector.tensor_copy, slice(HALF // 2, HALF))
 
         def w_stt(l, h, g):
             t, s = th[l, h, g], sg[l, h, g]
@@ -140,7 +168,7 @@ def tile_sparse_connect_kernel(tc, x_bytes, x_scale, th1, sign1, th2, sign2, rel
             wq[l, h, g], ws[l, h, g] = q, s
 
         def x_mul(i):
-            t = work.tile([P, D], BF16, name="xb", bufs=4, align_bytes=64)
+            t = work.tile([P, D], BF16, name="xb", bufs=6, align_bytes=64)
             nc.vector.tensor_tensor(out=t[:], in0=x8[:, i, :].bitcast(FP8), in1=scale[:], op=ALU.mult)
             xb[i] = t
 
@@ -155,7 +183,7 @@ def tile_sparse_connect_kernel(tc, x_bytes, x_scale, th1, sign1, th2, sign2, rel
         def x_exit(i, eng):
             i0, n = group[i]
             if i0 not in xg:
-                xg[i0] = work.tile([P, n, 2, P, 2], F32, name="xg", bufs=4, align_bytes=64)
+                xg[i0] = work.tile([P, n, 2, P, 2], F32, name="xg", bufs=6, align_bytes=64)
             dst = xg[i0][:, i - i0]
             src = xt[i][:].rearrange("p g u r -> p g r u")
             if eng == "S":
@@ -165,8 +193,8 @@ def tile_sparse_connect_kernel(tc, x_bytes, x_scale, th1, sign1, th2, sign2, rel
 
         def x_quant(i0):
             n = group[i0][1]
-            q = deep.tile([P, n, 2, P], U32, name="xq", bufs=4, align_bytes=64)
-            s = deep.tile([P, n, 2, P], U8, name="xs", bufs=4, align_bytes=64)
+            q = deep.tile([P, n, 2, P], U32, name="xq", bufs=8, align_bytes=64)
+            s = deep.tile([P, n, 2, P], U8, name="xs", bufs=8, align_bytes=64)
             nc.vector.quantize_mx(
                 out=q[:].rearrange("p c g r -> p (c g r)").bitcast(FP8X4),
                 scales=s[:].rearrange("p c g r -> p (c g r)"),
@@ -193,7 +221,7 @@ def tile_sparse_connect_kernel(tc, x_bytes, x_scale, th1, sign1, th2, sign2, rel
         def h_exit(i, h, eng):
             i0, n = group[i]
             if i0 not in hb:
-                hb[i0] = work.tile([P, n, 2, P, 4], BF16, name="hb", bufs=4, align_bytes=64)
+                hb[i0] = work.tile([P, n, 2, P, 4], BF16, name="hb", bufs=8, align_bytes=64)
             dst = hb[i0][:, i - i0, h]
             src = ht[i, h][:].rearrange("p t n -> p n t")
             if eng == "S":
@@ -228,18 +256,18 @@ def tile_sparse_connect_kernel(tc, x_bytes, x_scale, th1, sign1, th2, sign2, rel
             ot[i, n] = t
 
         def o_exit(i, n, eng):
-            if i not in ob:
-                ob[i] = work.tile([P, N], F32, name="ob", bufs=12, align_bytes=64)
-            dst = ob[i][:, n * HALF : (n + 1) * HALF]
+            ob[i, n] = work.tile([P, HALF], F32, name="ob", bufs=12, align_bytes=64)
+            dst = ob[i, n][:]
             if eng == "S":
                 nc.scalar.activation(out=dst, in_=ot[i, n][:], func=ACT.Relu)
             else:
                 nc.vector.tensor_scalar(out=dst, in0=ot[i, n][:], scalar1=0.0, scalar2=None, op0=ALU.max)
 
-        def store(i):
-            b, c = divmod(i, 4)
-            dst = out_rows[4 * b * P : (4 * b + 4) * P, :].rearrange("(p c) n -> c p n", c=4)[c]
-            nc.sync.dma_start(out=dst, in_=ob[i][:])
+        def store(i, n):
+            i0, c = [v for v in block.values() if v[0] <= i < v[0] + v[1]][0]
+            rows = out_rows[i0 * P : (i0 + c) * P, :].rearrange("(p c) n -> c p n", c=c)[i - i0]
+            nc.sync.dma_start(out=rows[:, n * HALF : (n + 1) * HALF], in_=ob[i, n][:])
+
         group = {}
         for i0, n in [(0,1),(1,1),(2,1),(3,1),(4,1),(5,1),(6,1),(7,1),(8,1),(9,1),(10,1),(11,1),(12,1),(13,1),(14,1),(15,1)]:
             for c in range(n):
@@ -248,30 +276,32 @@ def tile_sparse_connect_kernel(tc, x_bytes, x_scale, th1, sign1, th2, sign2, rel
             "r": w_relu, "m": w_prod, "i": w_ilv, "t": w_stt, "q": w_quant,
             "X": x_mul, "T": x_tr, "E": x_exit, "Q": x_quant,
             "A": l1, "H": h_exit, "K": h_quant, "B": l2, "O": o_exit, "S": store, "w1": load_w1, "w2": load_w2,
-            "s": load_scale, "p": spread_scale, "l": load_x, "v": w_ilv_vector,
+            "s": load_scale, "p": spread_scale, "l": load_x, "v": w_ilv_vector, "z": w_ilv_left, "y": w_ilv_right, "d": warm,
         }
         order = (
-            "s w1,0,0 l,0 w1,0,1 w1,1,0 w1,1,1 l,1 w2,0 w2,1 l,2 l,3 p r,1,0,0 m,1,0,0 i,1,0,0 X,2 r,1,0,1 "
-            "T,2 X,1 E,2,S m,1,0,1 T,1 E,1,S r,1,1,0 i,1,0,1 Q,2 m,1,1,0 Q,1 r,1,1,1 q,1,0,0 i,1,1,0 q,1,0,1 "
-            "m,1,1,1 A,1,0 A,2,0 X,5 i,1,1,1 q,1,1,0 T,5 r,2,1,0 X,6 E,5,S X,4 T,6 H,1,0,S E,6,S q,1,1,1 T,4 "
-            "H,2,0,S m,2,1,0 A,1,1 E,4,S A,2,1 r,2,1,1 H,1,1,S Q,4 i,2,1,0 Q,6 A,4,1 K,1 Q,5 A,4,0 r,2,0,1 "
-            "m,2,1,1 H,2,1,S q,2,1,0 H,4,1,S A,5,0 H,4,0,V i,2,1,1 A,6,0 X,12 A,5,1 X,13 T,12 H,5,1,S K,4 "
-            "T,13 q,2,1,1 H,6,0,S A,6,1 X,14 E,12,S E,13,S B,4,1 Q,12 B,1,1 H,6,1,S Q,13 A,12,0 O,4,1,S K,2 "
-            "K,6 O,1,1,S A,12,1 X,15 H,12,0,S B,2,1 H,12,1,S A,13,1 H,5,0,V O,2,1,S T,15 m,2,0,1 H,13,1,S "
-            "T,14 E,15,S K,12 B,6,1 K,5 E,14,S X,10 B,12,1 i,2,0,1 B,5,1 Q,15 A,13,0 Q,14 X,9 A,15,0 A,14,1 "
-            "X,11 H,13,0,S T,10 H,14,1,S T,9 K,13 H,15,0,S q,2,0,1 A,14,0 O,5,1,S E,9,V A,15,1 O,6,1,S "
-            "E,10,V B,13,1 H,14,0,S Q,9 T,11 H,15,1,S Q,10 K,14 A,9,0 O,13,1,S r,2,0,0 E,11,S B,14,1 K,15 "
-            "m,2,0,0 H,9,0,S A,9,1 O,14,1,S B,15,1 Q,11 H,9,1,S A,10,1 X,0 i,2,0,0 A,11,0 K,9 A,11,1 X,3 "
-            "B,9,1 T,0 O,9,1,V H,10,1,S T,3 q,2,0,0 E,0,S A,10,0 H,11,1,V O,15,1,S B,12,0 Q,0 H,11,0,S "
-            "H,10,0,V B,15,0 E,3,S O,12,0,V A,0,0 O,15,0,S S,15 K,10 B,13,0 K,11 O,12,1,S S,12 Q,3 B,10,0 "
-            "X,8 H,0,0,S A,3,1 O,10,0,S B,9,0 O,13,0,V S,13 H,3,1,S B,4,0 X,7 O,9,0,S S,9 B,6,0 O,4,0,S S,4 "
-            "B,11,0 O,6,0,S S,6 B,1,0 O,11,0,S A,3,0 O,1,0,S S,1 B,11,1 H,3,0,S B,2,0 O,11,1,S S,11 B,14,0 "
-            "K,3 O,2,0,V S,2 B,10,1 O,14,0,S S,14 B,3,0 O,10,1,V S,10 B,3,1 O,3,0,S T,7 O,3,1,V S,3 T,8 "
-            "E,7,V B,5,0 E,8,S Q,7 A,0,1 O,5,0,V S,5 A,7,0 Q,8 H,0,1,V A,7,1 H,7,0,S A,8,0 K,0 H,7,1,S A,8,1 "
-            "H,8,0,S K,7 B,0,0 H,8,1,V B,0,1 O,0,0,V B,7,0 O,0,1,S S,0 K,8 B,7,1 O,7,0,V B,8,1 O,7,1,S S,7 "
-            "B,8,0 O,8,1,S O,8,0,S S,8 "
+            "s w1,0,0 l,0,2 w1,0,1 l,2,2 w1,1,0 w1,1,1 l,4,4 w2,0 w2,1 l,8,4 l,12,4 d,4 p r,1,0,0 m,1,0,0 "
+            "X,1 i,1,0,0 X,0 T,1 r,1,0,1 T,0 E,1,S m,1,0,1 E,0,S X,2 i,1,0,1 Q,1 T,2 r,1,1,0 Q,0 m,1,1,0 "
+            "E,2,S q,1,0,1 i,1,1,0 Q,2 q,1,0,0 r,1,1,1 A,1,0 X,3 A,0,0 H,1,0,S A,2,0 X,5 H,0,0,S T,3 H,2,0,S "
+            "m,1,1,1 T,5 E,3,S E,5,S Q,3 X,4 i,1,1,1 A,3,0 Q,5 T,4 X,6 A,5,0 q,1,1,0 T,6 H,3,0,S q,1,1,1 "
+            "H,5,0,S X,7 A,1,1 E,6,S E,4,S A,5,1 Q,6 H,1,1,S r,2,0,0 A,0,1 H,5,1,S Q,4 A,6,0 m,2,0,0 H,0,1,S "
+            "A,6,1 H,6,0,S A,4,1 K,0 H,6,1,S X,11 A,2,1 i,2,0,0 A,3,1 X,13 T,11 T,7 X,10 H,3,1,S K,1 E,7,S "
+            "A,4,0 K,3 E,11,S X,14 T,10 H,4,0,S T,13 E,10,S Q,11 Q,7 T,14 E,13,S X,9 H,2,1,S A,7,1 E,14,S "
+            "Q,10 A,7,0 Q,13 H,7,1,S K,2 T,9 Q,14 H,7,0,S K,5 A,10,0 E,9,S r,2,0,1 A,14,1 H,4,1,S K,7 "
+            "m,2,0,1 A,14,0 H,10,0,S H,14,1,S A,10,1 K,4 H,14,0,S v,2,0,1 A,13,0 H,10,1,S A,11,1 H,13,0,S "
+            "A,13,1 Q,9 H,11,1,S q,2,0,1 A,11,0 H,13,1,S K,14 A,9,1 q,2,0,0 H,11,0,S A,9,0 K,13 H,9,1,S K,11 "
+            "B,2,0 H,9,0,S r,2,1,1 B,0,0 O,2,0,S S,2,0 X,8 B,11,0 O,0,0,S S,0,0 B,7,0 K,9 O,11,0,S S,11,0 "
+            "B,13,0 X,12 O,7,0,S S,7,0 B,9,0 O,13,0,S S,13,0 T,8 m,2,1,1 O,9,0,S S,9,0 T,12 E,8,S K,10 "
+            "B,14,0 i,2,1,1 E,12,V B,10,0 Q,8 r,2,1,0 B,3,0 A,8,1 Q,12 m,2,1,0 A,8,0 O,10,0,S S,10,0 A,12,0 "
+            "O,14,0,S S,14,0 q,2,1,1 B,4,0 O,3,0,S S,3,0 v,2,1,0 B,1,0 H,12,0,S B,5,0 O,4,0,S S,4,0 A,12,1 "
+            "K,6 O,5,0,S S,5,0 q,2,1,0 B,6,0 O,1,0,S S,1,0 H,12,1,V B,1,1 H,8,1,S O,6,0,V S,6,0 B,7,1 "
+            "O,1,1,S S,1,1 K,12 B,10,1 X,15 O,7,1,S S,7,1 B,12,0 O,10,1,S S,10,1 B,4,1 H,8,0,V O,12,0,S "
+            "S,12,0 B,12,1 O,4,1,S S,4,1 K,8 B,13,1 O,12,1,V S,12,1 B,8,1 O,13,1,V S,13,1 B,2,1 O,8,1,S "
+            "S,8,1 B,6,1 O,2,1,S S,2,1 B,11,1 O,6,1,V S,6,1 T,15 O,11,1,V S,11,1 B,0,1 E,15,S B,5,1 O,0,1,S "
+            "S,0,1 Q,15 B,9,1 O,5,1,S S,5,1 A,15,0 O,9,1,V S,9,1 A,15,1 H,15,0,S B,3,1 H,15,1,V B,8,0 "
+            "O,3,1,S S,3,1 K,15 B,14,1 O,8,0,S S,8,0 B,15,0 O,14,1,S S,14,1 B,15,1 O,15,0,V S,15,0 O,15,1,S "
+            "S,15,1 "
         )
         with tc.manual_schedule():
             for token in order.split():
-                parts = token.split(",")
-                run[parts[0]](*[a if a in "SV" else int(a) for a in parts[1:]])
+                field = token.split(",")
+                run[field[0]](*[a if a in "SV" else int(a) for a in field[1:]])

@@ -3,8 +3,8 @@ from contextlib import ExitStack
 import concourse.mybir as mybir
 from concourse.masks import make_identity
 
-TOK, D, F, N = 2048, 1024, 1024, 1024
-FLOPS = 2 * TOK * D * F + 2 * TOK * F * N
+TOKENS, D, F, N = 2048, 1024, 1024, 1024
+FLOPS = 2 * TOKENS * D * F + 2 * TOKENS * F * N
 
 F32 = mybir.dt.float32
 BF16 = mybir.dt.bfloat16
@@ -12,296 +12,331 @@ U32 = mybir.dt.uint32
 U8 = mybir.dt.uint8
 FP8 = mybir.dt.float8_e4m3fn
 FP8X4 = mybir.dt.float8_e4m3fn_x4
-ALU = mybir.AluOpType
-ACT = mybir.ActivationFunctionType
+MAX = mybir.AluOpType.max
+MULT = mybir.AluOpType.mult
+RELU = mybir.ActivationFunctionType.Relu
+
 P = 128
-HALF = 512
+PACK = 4
+HALF = P * PACK
+
+LOADS = ((0, 2), (2, 2), (4, 4), (8, 4), (12, 4))
+GROUPS = ((0, 1), (1, 1), (2, 2), (4, 2), (6, 2), (8, 2), (10, 2), (12, 1), (13, 2), (15, 1))
 
 
 def tile_sparse_connect_kernel(tc, x_bytes, x_scale, th1, sign1, th2, sign2, relu, out):
+    assert relu == 1
     nc = tc.nc
     x_rows = x_bytes.flatten_outer_dims()
     out_rows = out.flatten_outer_dims()
-    raw = {
-        1: [a.rearrange("(g p j) f -> g p j f", p=P, j=4) for a in (th1, sign1)],
-        2: [a.rearrange("(g p j) f -> g p j f", p=P, j=4) for a in (th2, sign2)],
-    }
+    w1_hbm = [a.rearrange("(g p j) f -> g p j f", p=P, j=PACK) for a in (th1, sign1)]
+    w2_hbm = [a.rearrange("(g p j) f -> g p j f", p=P, j=PACK) for a in (th2, sign2)]
+    group_size = dict(GROUPS)
+
     with ExitStack() as ctx:
         keep = ctx.enter_context(tc.tile_pool(name="keep", bufs=1))
-        rawp = ctx.enter_context(tc.tile_pool(name="rawp", bufs=4))
-        grp = ctx.enter_context(tc.tile_pool(name="grp", bufs=3))
+        stage = ctx.enter_context(tc.tile_pool(name="stage", bufs=4))
         work = ctx.enter_context(tc.tile_pool(name="work", bufs=6))
-        deep = ctx.enter_context(tc.tile_pool(name="deep", bufs=16))
-        px = ctx.enter_context(tc.psum_pool(name="px", bufs=2))
-        ph = ctx.enter_context(tc.psum_pool(name="ph", bufs=3))
-        po = ctx.enter_context(tc.psum_pool(name="po", bufs=3))
+        psum = ctx.enter_context(tc.psum_pool(name="psum", bufs=8))
 
-        ident = keep.tile([P, P], F32)
-        make_identity(nc, ident[:])
+        identity = keep.tile([P, P], F32)
+        make_identity(nc, identity[:])
+        scale_column = keep.tile([P, 8], F32, align_bytes=64)
         scale = keep.tile([P, D], F32, align_bytes=64)
-        s8 = keep.tile([P, 8], F32, align_bytes=64)
-        th, sg, wg, wq, ws = {}, {}, {}, {}, {}
-        block = {}
-        x8 = keep.tile([P, 16, D], U8, align_bytes=64)
-        xb, xt, xg, xq, xs, ht, hb, hq, hs, ot, ob = {}, {}, {}, {}, {}, {}, {}, {}, {}, {}, {}
+        x_codes_in = keep.tile([P, TOKENS // P, D], U8, align_bytes=64)
 
-        def parts(l, h, g):
-            return (slice(0, 2), slice(2, 4)) if (l, h, g) == (1, 0, 0) else (slice(0, 4),)
+        theta, sign, grouped, w_codes, w_scales = {}, {}, {}, {}, {}
+        x_tok, x_turned, x_grouped, x_codes, x_scales = {}, {}, {}, {}, {}
+        h_grouped, h_codes, h_scales = {}, {}, {}
 
-        def load_w1(h, g):
-            cols = slice(h * HALF, (h + 1) * HALF)
-            t = rawp.tile([P, 4, HALF], BF16, name="th1_raw", align_bytes=64)
-            s = rawp.tile([P, 4, HALF], BF16, name="sg1_raw", align_bytes=64)
-            for dst, src in ((t, raw[1][0][g]), (s, raw[1][1][g])):
-                for rows in parts(1, h, g):
+        def tiles_of(group):
+            return range(group, group + group_size[group])
+
+
+        def row_parts(layer, half, g):
+            return (slice(0, 2), slice(2, 4)) if (layer, half, g) == (1, 0, 0) else (slice(0, 4),)
+
+        def load_w1(half, g):
+            cols = slice(half * HALF, (half + 1) * HALF)
+            th = stage.tile([P, PACK, HALF], BF16, name="theta1", align_bytes=64)
+            sg = stage.tile([P, PACK, HALF], BF16, name="sign1", align_bytes=64)
+            for dst, src in ((th, w1_hbm[0][g]), (sg, w1_hbm[1][g])):
+                for rows in row_parts(1, half, g):
                     nc.sync.dma_start(out=dst[:, rows], in_=src[:, rows, cols])
-            th[1, h, g], sg[1, h, g] = t[:], s[:]
+            theta[1, half, g], sign[1, half, g] = th[:], sg[:]
 
         def load_w2(g):
-            t = rawp.tile([P, 4, N], BF16, name="th2_raw", bufs=2, align_bytes=64)
-            nc.sync.dma_start(out=t[:], in_=raw[2][0][g])
-            s = rawp.tile([P, 4, N], BF16, name="sg2_raw", bufs=2, align_bytes=64)
-            nc.sync.dma_start(out=s[:], in_=raw[2][1][g])
-            for h in (0, 1):
-                cols = slice(h * HALF, (h + 1) * HALF)
-                th[2, h, g], sg[2, h, g] = t[:, :, cols], s[:, :, cols]
+            th = stage.tile([P, PACK, N], BF16, name="theta2", bufs=2, align_bytes=64)
+            nc.sync.dma_start(out=th[:], in_=w2_hbm[0][g])
+            sg = stage.tile([P, PACK, N], BF16, name="sign2", bufs=2, align_bytes=64)
+            nc.sync.dma_start(out=sg[:], in_=w2_hbm[1][g])
+            for half in (0, 1):
+                cols = slice(half * HALF, (half + 1) * HALF)
+                theta[2, half, g], sign[2, half, g] = th[:, :, cols], sg[:, :, cols]
 
-        def load_scale():
-            nc.scalar.dma_start(out=s8[:], in_=x_scale.rearrange("a b (p c) -> p (a b c)", c=8))
+        def load_x(first, count):
+            nc.sync.dma_start(
+                out=x_codes_in[:, first : first + count],
+                in_=x_rows[first * P : (first + count) * P, :].rearrange("(p c) d -> p c d", c=count),
+            )
 
         def spread_scale():
             for b in (0, 1):
-                t = po.tile([P, HALF], F32, name="ot")
-                for c in range(4):
-                    k = 4 * b + c
+                bank = psum.tile([P, PACK, P], F32, name="scale_bank", tag="bank")
+                for c in range(PACK):
+                    column = scale_column[:, PACK * b + c : PACK * b + c + 1]
                     nc.tensor.matmul(
-                        out=t[:, c * P : (c + 1) * P],
-                        lhsT=s8[:, k : k + 1].to_broadcast([P, P]),
-                        rhs=ident[:],
-                        start=True,
-                        stop=True,
+                        out=bank[:, c], lhsT=column.to_broadcast([P, P]), rhs=identity[:], start=True, stop=True
                     )
                 nc.scalar.copy(
-                    out=scale[:].rearrange("p (q c) -> p q c", c=8)[:, :, 4 * b : 4 * b + 4],
-                    in_=t[:].rearrange("p (c q) -> p q c", c=4),
+                    out=scale[:].rearrange("p (q c) -> p q c", c=8)[:, :, PACK * b : PACK * (b + 1)],
+                    in_=bank[:].rearrange("p c q -> p q c"),
                 )
 
-        def load_x(i, n):
-            block[i] = (i, n)
-            nc.sync.dma_start(
-                out=x8[:, i : i + n, :],
-                in_=x_rows[i * P : (i + n) * P, :].rearrange("(p c) d -> p c d", c=n),
-            )
 
-        def warm(n):
-            t = po.tile([P, HALF], F32, name="ot")
-            for c in range(n):
-                nc.tensor.matmul(out=t[:, c * P : (c + 1) * P], lhsT=ident[:], rhs=ident[:], start=True, stop=True)
+        def relu_w(layer, half, g):
+            th = theta[layer, half, g]
+            for rows in row_parts(layer, half, g):
+                nc.vector.tensor_scalar(out=th[:, rows], in0=th[:, rows], scalar1=0.0, scalar2=None, op0=MAX)
 
-        def w_relu(l, h, g):
-            t = th[l, h, g]
-            for rows in parts(l, h, g):
-                nc.vector.tensor_scalar(out=t[:, rows], in0=t[:, rows], scalar1=0.0, scalar2=None, op0=ALU.max)
+        def sign_w(layer, half, g):
+            th, sg = theta[layer, half, g], sign[layer, half, g]
+            for rows in row_parts(layer, half, g):
+                nc.vector.tensor_tensor(out=th[:, rows], in0=th[:, rows], in1=sg[:, rows], op=MULT)
 
-        def w_prod(l, h, g):
-            t, s = th[l, h, g], sg[l, h, g]
-            for rows in parts(l, h, g):
-                nc.vector.tensor_tensor(out=t[:, rows], in0=t[:, rows], in1=s[:, rows], op=ALU.mult)
-
-        def w_ilv_part(l, h, g, copy, part):
-            if (l, h, g) not in wg:
-                wg[l, h, g] = grp.tile([P, 4 * HALF], BF16, name="w_grouped", align_bytes=64)
-            w = wg[l, h, g]
-            if l == 1:
-                sel = slice(4 * part.start // HALF, 4 * part.stop // HALF)
+        def interleave_w(layer, half, g, copy):
+            w = stage.tile([P, HALF * PACK], BF16, name="w_grouped", bufs=3, align_bytes=64)
+            th = theta[layer, half, g]
+            if layer == 1:
                 copy(
-                    out=w[:].rearrange("p (t m j) -> p m t j", t=4, j=4)[:, :, sel],
-                    in_=th[l, h, g].rearrange("p j (m t) -> p m t j", t=4)[:, :, sel],
+                    out=w[:].rearrange("p (t m j) -> p m t j", t=PACK, j=PACK),
+                    in_=th.rearrange("p j (m t) -> p m t j", t=PACK),
                 )
             else:
-                cols = slice(part.start // 4, part.stop // 4)
                 copy(
-                    out=w[:].rearrange("p (c i j) -> p c j i", i=4, j=4)[:, cols],
-                    in_=th[l, h, g].rearrange("p j (c i) -> p c j i", i=4)[:, cols],
+                    out=w[:].rearrange("p (c i j) -> p c j i", i=4, j=PACK),
+                    in_=th.rearrange("p j (c i) -> p c j i", i=4),
                 )
+            grouped[layer, half, g] = w
 
-        def w_ilv(l, h, g):
-            w_ilv_part(l, h, g, nc.scalar.copy, slice(0, HALF))
+        def quantize_w(layer, half, g):
+            codes = keep.tile([P, HALF], U32, name=f"w_codes{layer}{half}{g}", align_bytes=64)
+            scales = keep.tile([P, HALF], U8, name=f"w_scales{layer}{half}{g}", align_bytes=64)
+            nc.vector.quantize_mx(out=codes[:].bitcast(FP8X4), scales=scales[:], in_=grouped[layer, half, g][:])
+            w_codes[layer, half, g], w_scales[layer, half, g] = codes, scales
 
-        def w_ilv_vector(l, h, g):
-            w_ilv_part(l, h, g, nc.vector.tensor_copy, slice(0, HALF))
 
-        def w_ilv_left(l, h, g):
-            w_ilv_part(l, h, g, nc.scalar.copy, slice(0, HALF // 2))
+        def multiply_x(i):
+            t = work.tile([P, D], BF16, name="x_tok", align_bytes=64)
+            nc.vector.tensor_tensor(out=t[:], in0=x_codes_in[:, i].bitcast(FP8), in1=scale[:], op=MULT)
+            x_tok[i] = t
 
-        def w_ilv_right(l, h, g):
-            w_ilv_part(l, h, g, nc.vector.tensor_copy, slice(HALF // 2, HALF))
-
-        def w_stt(l, h, g):
-            t, s = th[l, h, g], sg[l, h, g]
-            w = grp.tile([P, 4 * HALF], BF16, name="w_grouped", align_bytes=64)
-            wg[l, h, g] = w
-            if l == 1:
-                for k in range(4):
-                    nc.vector.scalar_tensor_tensor(
-                        out=w[:].rearrange("p (t m j) -> p t m j", t=4, j=4)[:, k],
-                        in0=t.rearrange("p j (m t) -> p t m j", t=4)[:, k],
-                        scalar=0.0,
-                        in1=s.rearrange("p j (m t) -> p t m j", t=4)[:, k],
-                        op0=ALU.max,
-                        op1=ALU.mult,
-                    )
-            else:
-                nc.vector.scalar_tensor_tensor(
-                    out=w[:].rearrange("p (n j) -> p n j", j=4),
-                    in0=t.rearrange("p j n -> p n j"),
-                    scalar=0.0,
-                    in1=s.rearrange("p j n -> p n j"),
-                    op0=ALU.max,
-                    op1=ALU.mult,
-                )
-
-        def w_quant(l, h, g):
-            q = keep.tile([P, HALF], U32, name=f"wq{l}{h}{g}", align_bytes=64)
-            s = keep.tile([P, HALF], U8, name=f"ws{l}{h}{g}", align_bytes=64)
-            nc.vector.quantize_mx(out=q[:].bitcast(FP8X4), scales=s[:], in_=wg[l, h, g][:])
-            wq[l, h, g], ws[l, h, g] = q, s
-
-        def x_mul(i):
-            t = work.tile([P, D], BF16, name="xb", bufs=6, align_bytes=64)
-            nc.vector.tensor_tensor(out=t[:], in0=x8[:, i, :].bitcast(FP8), in1=scale[:], op=ALU.mult)
-            xb[i] = t
-
-        def x_tr(i):
-            t = px.tile([P, 2, 2, P], F32, name="xt")
-            words = xb[i][:].bitcast(F32)
+        def turn_x(i):
+            words = x_tok[i][:].bitcast(F32)
+            bank = psum.tile([P, 2, 2, P], F32, name="x_bank", tag="bank")
             for g in (0, 1):
                 for u in (0, 1):
-                    nc.tensor.transpose(t[:, g, u, :], words[:, 256 * g + u : 256 * (g + 1) : 2], ident[:])
-            xt[i] = t
+                    nc.tensor.transpose(bank[:, g, u], words[:, 256 * g + u : 256 * (g + 1) : 2], identity[:])
+            group = max(first for first, _ in GROUPS if first <= i)
+            if i == group:
+                x_grouped[group] = work.tile([P, group_size[group], 2, P, 2], F32, name="x_grouped", bufs=4, align_bytes=64)
+            nc.scalar.copy(out=x_grouped[group][:, i - group], in_=bank[:].rearrange("p g u r -> p g r u"))
 
-        def x_exit(i, eng):
-            i0, n = group[i]
-            if i0 not in xg:
-                xg[i0] = work.tile([P, n, 2, P, 2], F32, name="xg", bufs=6, align_bytes=64)
-            dst = xg[i0][:, i - i0]
-            src = xt[i][:].rearrange("p g u r -> p g r u")
-            if eng == "S":
-                nc.scalar.copy(out=dst, in_=src)
-            else:
-                nc.vector.tensor_copy(out=dst, in_=src)
-
-        def x_quant(i0):
-            n = group[i0][1]
-            q = deep.tile([P, n, 2, P], U32, name="xq", bufs=8, align_bytes=64)
-            s = deep.tile([P, n, 2, P], U8, name="xs", bufs=8, align_bytes=64)
+        def quantize_x(group):
+            count = group_size[group]
+            codes = work.tile([P, count, 2, P], U32, name="x_codes", bufs=6, align_bytes=64)
+            scales = work.tile([P, count, 2, P], U8, name="x_scales", bufs=6, align_bytes=64)
             nc.vector.quantize_mx(
-                out=q[:].rearrange("p c g r -> p (c g r)").bitcast(FP8X4),
-                scales=s[:].rearrange("p c g r -> p (c g r)"),
-                in_=xg[i0][:].rearrange("p c g r u -> p (c g r u)").bitcast(BF16),
+                out=codes[:].rearrange("p c g r -> p (c g r)").bitcast(FP8X4),
+                scales=scales[:].rearrange("p c g r -> p (c g r)"),
+                in_=x_grouped[group][:].rearrange("p c g r u -> p (c g r u)").bitcast(BF16),
             )
-            for c in range(n):
-                xq[i0 + c], xs[i0 + c] = q[:, c], s[:, c]
+            for c, i in enumerate(tiles_of(group)):
+                x_codes[i], x_scales[i] = codes[:, c], scales[:, c]
 
-        def l1(i, h):
-            t = ph.tile([P, 4, P], F32, name="ht")
-            for k in range(4):
+
+        def layer1(group, half):
+            if half == 0:
+                h_grouped[group] = work.tile(
+                    [P, group_size[group], 2, P, PACK], BF16, name="h_grouped", bufs=7, align_bytes=64
+                )
+            for c, i in enumerate(tiles_of(group)):
+                bank = psum.tile([P, PACK, P], F32, name="h_bank", tag="bank")
+                for t in range(PACK):
+                    cols = slice(t * P, (t + 1) * P)
+                    for g in (0, 1):
+                        nc.tensor.matmul_mx(
+                            out=bank[:, t],
+                            lhsT=w_codes[1, half, g][:, cols].bitcast(FP8X4),
+                            lhsT_scale=w_scales[1, half, g][:, cols],
+                            rhs=x_codes[i][:, g].bitcast(FP8X4),
+                            rhs_scale=x_scales[i][:, g],
+                            start=(g == 0),
+                            stop=(g == 1),
+                        )
+                nc.scalar.activation(
+                    out=h_grouped[group][:, c, half], in_=bank[:].rearrange("p t n -> p n t"), func=RELU
+                )
+
+        def quantize_h(group):
+            count = group_size[group]
+            codes = work.tile([P, count, 2, P], U32, name="h_codes", bufs=len(GROUPS), align_bytes=64)
+            scales = work.tile([P, count, 2, P], U8, name="h_scales", bufs=len(GROUPS), align_bytes=64)
+            nc.vector.quantize_mx(
+                out=codes[:].rearrange("p c g n -> p (c g n)").bitcast(FP8X4),
+                scales=scales[:].rearrange("p c g n -> p (c g n)"),
+                in_=h_grouped[group][:].rearrange("p c g n t -> p (c g n t)"),
+            )
+            for c, i in enumerate(tiles_of(group)):
+                h_codes[i], h_scales[i] = codes[:, c], scales[:, c]
+
+
+        def layer2(group, half, vector_tiles=()):
+            cols = slice(half * HALF, (half + 1) * HALF)
+            for i in tiles_of(group):
+                bank = psum.tile([P, HALF], F32, name="out_bank", tag="bank")
                 for g in (0, 1):
                     nc.tensor.matmul_mx(
-                        out=t[:, k, :],
-                        lhsT=wq[1, h, g][:, k * P : (k + 1) * P].bitcast(FP8X4),
-                        lhsT_scale=ws[1, h, g][:, k * P : (k + 1) * P],
-                        rhs=xq[i][:, g].bitcast(FP8X4),
-                        rhs_scale=xs[i][:, g],
+                        out=bank[:],
+                        lhsT=h_codes[i][:, g].bitcast(FP8X4),
+                        lhsT_scale=h_scales[i][:, g],
+                        rhs=w_codes[2, half, g][:].bitcast(FP8X4),
+                        rhs_scale=w_scales[2, half, g][:],
                         start=(g == 0),
                         stop=(g == 1),
                     )
-            ht[i, h] = t
+                result = work.tile([P, HALF], F32, name="result", bufs=8, align_bytes=64)
+                if i in vector_tiles:
+                    nc.vector.tensor_scalar(out=result[:], in0=bank[:], scalar1=0.0, scalar2=None, op0=MAX)
+                else:
+                    nc.scalar.activation(out=result[:], in_=bank[:], func=RELU)
+                first, count = max(load for load in LOADS if load[0] <= i)
+                rows = out_rows[first * P : (first + count) * P, :].rearrange("(p c) n -> c p n", c=count)
+                nc.sync.dma_start(out=rows[i - first][:, cols], in_=result[:])
 
-        def h_exit(i, h, eng):
-            i0, n = group[i]
-            if i0 not in hb:
-                hb[i0] = work.tile([P, n, 2, P, 4], BF16, name="hb", bufs=8, align_bytes=64)
-            dst = hb[i0][:, i - i0, h]
-            src = ht[i, h][:].rearrange("p t n -> p n t")
-            if eng == "S":
-                nc.scalar.activation(out=dst, in_=src, func=ACT.Relu)
-            else:
-                nc.vector.tensor_scalar(out=dst, in0=src, scalar1=0.0, scalar2=None, op0=ALU.max)
 
-        def h_quant(i0):
-            n = group[i0][1]
-            q = deep.tile([P, n, 2, P], U32, name="hq", align_bytes=64)
-            s = deep.tile([P, n, 2, P], U8, name="hs", align_bytes=64)
-            nc.vector.quantize_mx(
-                out=q[:].rearrange("p c h r -> p (c h r)").bitcast(FP8X4),
-                scales=s[:].rearrange("p c h r -> p (c h r)"),
-                in_=hb[i0][:].rearrange("p c h r t -> p (c h r t)"),
-            )
-            for c in range(n):
-                hq[i0 + c], hs[i0 + c] = q[:, c], s[:, c]
+        scalar_copy, vector_copy = nc.scalar.copy, nc.vector.tensor_copy
 
-        def l2(i, n):
-            t = po.tile([P, HALF], F32, name="ot")
-            for h in (0, 1):
-                nc.tensor.matmul_mx(
-                    out=t[:],
-                    lhsT=hq[i][:, h].bitcast(FP8X4),
-                    lhsT_scale=hs[i][:, h],
-                    rhs=wq[2, n, h][:].bitcast(FP8X4),
-                    rhs_scale=ws[2, n, h][:],
-                    start=(h == 0),
-                    stop=(h == 1),
-                )
-            ot[i, n] = t
-
-        def o_exit(i, n, eng):
-            ob[i, n] = work.tile([P, HALF], F32, name="ob", bufs=12, align_bytes=64)
-            dst = ob[i, n][:]
-            if eng == "S":
-                nc.scalar.activation(out=dst, in_=ot[i, n][:], func=ACT.Relu)
-            else:
-                nc.vector.tensor_scalar(out=dst, in0=ot[i, n][:], scalar1=0.0, scalar2=None, op0=ALU.max)
-
-        def store(i, n):
-            i0, c = [v for v in block.values() if v[0] <= i < v[0] + v[1]][0]
-            rows = out_rows[i0 * P : (i0 + c) * P, :].rearrange("(p c) n -> c p n", c=c)[i - i0]
-            nc.sync.dma_start(out=rows[:, n * HALF : (n + 1) * HALF], in_=ob[i, n][:])
-
-        group = {}
-        for i0, n in [(0,1),(1,1),(2,1),(3,1),(4,1),(5,1),(6,1),(7,1),(8,1),(9,1),(10,1),(11,1),(12,1),(13,1),(14,1),(15,1)]:
-            for c in range(n):
-                group[i0 + c] = (i0, n)
-        run = {
-            "r": w_relu, "m": w_prod, "i": w_ilv, "t": w_stt, "q": w_quant,
-            "X": x_mul, "T": x_tr, "E": x_exit, "Q": x_quant,
-            "A": l1, "H": h_exit, "K": h_quant, "B": l2, "O": o_exit, "S": store, "w1": load_w1, "w2": load_w2,
-            "s": load_scale, "p": spread_scale, "l": load_x, "v": w_ilv_vector, "z": w_ilv_left, "y": w_ilv_right, "d": warm,
-        }
-        order = (
-            "s w1,0,0 l,0,2 w1,0,1 l,2,2 w1,1,0 w1,1,1 l,4,4 w2,0 w2,1 l,8,4 l,12,4 d,4 p r,1,0,0 m,1,0,0 "
-            "X,1 i,1,0,0 X,0 T,1 r,1,0,1 T,0 E,1,S m,1,0,1 E,0,S X,2 i,1,0,1 Q,1 T,2 r,1,1,0 Q,0 m,1,1,0 "
-            "E,2,S q,1,0,1 i,1,1,0 Q,2 q,1,0,0 r,1,1,1 A,1,0 X,3 A,0,0 H,1,0,S A,2,0 X,5 H,0,0,S T,3 H,2,0,S "
-            "m,1,1,1 T,5 E,3,S E,5,S Q,3 X,4 i,1,1,1 A,3,0 Q,5 T,4 X,6 A,5,0 q,1,1,0 T,6 H,3,0,S q,1,1,1 "
-            "H,5,0,S X,7 A,1,1 E,6,S E,4,S A,5,1 Q,6 H,1,1,S r,2,0,0 A,0,1 H,5,1,S Q,4 A,6,0 m,2,0,0 H,0,1,S "
-            "A,6,1 H,6,0,S A,4,1 K,0 H,6,1,S X,11 A,2,1 i,2,0,0 A,3,1 X,13 T,11 T,7 X,10 H,3,1,S K,1 E,7,S "
-            "A,4,0 K,3 E,11,S X,14 T,10 H,4,0,S T,13 E,10,S Q,11 Q,7 T,14 E,13,S X,9 H,2,1,S A,7,1 E,14,S "
-            "Q,10 A,7,0 Q,13 H,7,1,S K,2 T,9 Q,14 H,7,0,S K,5 A,10,0 E,9,S r,2,0,1 A,14,1 H,4,1,S K,7 "
-            "m,2,0,1 A,14,0 H,10,0,S H,14,1,S A,10,1 K,4 H,14,0,S v,2,0,1 A,13,0 H,10,1,S A,11,1 H,13,0,S "
-            "A,13,1 Q,9 H,11,1,S q,2,0,1 A,11,0 H,13,1,S K,14 A,9,1 q,2,0,0 H,11,0,S A,9,0 K,13 H,9,1,S K,11 "
-            "B,2,0 H,9,0,S r,2,1,1 B,0,0 O,2,0,S S,2,0 X,8 B,11,0 O,0,0,S S,0,0 B,7,0 K,9 O,11,0,S S,11,0 "
-            "B,13,0 X,12 O,7,0,S S,7,0 B,9,0 O,13,0,S S,13,0 T,8 m,2,1,1 O,9,0,S S,9,0 T,12 E,8,S K,10 "
-            "B,14,0 i,2,1,1 E,12,V B,10,0 Q,8 r,2,1,0 B,3,0 A,8,1 Q,12 m,2,1,0 A,8,0 O,10,0,S S,10,0 A,12,0 "
-            "O,14,0,S S,14,0 q,2,1,1 B,4,0 O,3,0,S S,3,0 v,2,1,0 B,1,0 H,12,0,S B,5,0 O,4,0,S S,4,0 A,12,1 "
-            "K,6 O,5,0,S S,5,0 q,2,1,0 B,6,0 O,1,0,S S,1,0 H,12,1,V B,1,1 H,8,1,S O,6,0,V S,6,0 B,7,1 "
-            "O,1,1,S S,1,1 K,12 B,10,1 X,15 O,7,1,S S,7,1 B,12,0 O,10,1,S S,10,1 B,4,1 H,8,0,V O,12,0,S "
-            "S,12,0 B,12,1 O,4,1,S S,4,1 K,8 B,13,1 O,12,1,V S,12,1 B,8,1 O,13,1,V S,13,1 B,2,1 O,8,1,S "
-            "S,8,1 B,6,1 O,2,1,S S,2,1 B,11,1 O,6,1,V S,6,1 T,15 O,11,1,V S,11,1 B,0,1 E,15,S B,5,1 O,0,1,S "
-            "S,0,1 Q,15 B,9,1 O,5,1,S S,5,1 A,15,0 O,9,1,V S,9,1 A,15,1 H,15,0,S B,3,1 H,15,1,V B,8,0 "
-            "O,3,1,S S,3,1 K,15 B,14,1 O,8,0,S S,8,0 B,15,0 O,14,1,S S,14,1 B,15,1 O,15,0,V S,15,0 O,15,1,S "
-            "S,15,1 "
-        )
         with tc.manual_schedule():
-            for token in order.split():
-                field = token.split(",")
-                run[field[0]](*[a if a in "SV" else int(a) for a in field[1:]])
+            nc.scalar.dma_start(out=scale_column[:], in_=x_scale.rearrange("a b (p c) -> p (a b c)", c=8))
+            load_w1(0, 0)
+            load_x(*LOADS[0])
+            load_w1(0, 1)
+            load_x(*LOADS[1])
+            load_w1(1, 0)
+            load_w1(1, 1)
+            load_x(*LOADS[2])
+            load_w2(0)
+            load_w2(1)
+            load_x(*LOADS[3])
+            load_x(*LOADS[4])
+            spread_scale()
+
+            relu_w(1, 0, 0)
+            sign_w(1, 0, 0)
+            interleave_w(1, 0, 0, scalar_copy)
+            relu_w(1, 0, 1)
+            multiply_x(0)
+            turn_x(0)
+            sign_w(1, 0, 1)
+            interleave_w(1, 0, 1, scalar_copy)
+            multiply_x(1)
+            turn_x(1)
+            relu_w(1, 1, 0)
+            multiply_x(2)
+            turn_x(2)
+            quantize_x(0)
+            sign_w(1, 1, 0)
+            interleave_w(1, 1, 0, scalar_copy)
+            relu_w(1, 1, 1)
+            multiply_x(3)
+            sign_w(1, 1, 1)
+            interleave_w(1, 1, 1, scalar_copy)
+            turn_x(3)
+            multiply_x(4)
+            turn_x(4)
+            quantize_w(1, 0, 0)
+            quantize_w(1, 0, 1)
+            multiply_x(5)
+            turn_x(5)
+            layer1(0, 0)
+            for i in (6, 7):
+                multiply_x(i)
+                turn_x(i)
+            quantize_x(1)
+            quantize_x(2)
+            quantize_w(1, 1, 0)
+            quantize_w(1, 1, 1)
+
+            layer1(1, 0)
+            layer1(2, 0)
+            relu_w(2, 0, 0)
+            quantize_x(4)
+            layer1(0, 1)
+            layer1(1, 1)
+            sign_w(2, 0, 0)
+            interleave_w(2, 0, 0, scalar_copy)
+            layer1(2, 1)
+            quantize_x(6)
+            layer1(4, 0)
+            layer1(4, 1)
+            for i in range(8, 12):
+                multiply_x(i)
+                turn_x(i)
+            layer1(6, 0)
+            layer1(6, 1)
+            for i in range(12, 16):
+                multiply_x(i)
+                turn_x(i)
+            quantize_x(8)
+            relu_w(2, 0, 1)
+            quantize_h(0)
+            quantize_h(1)
+            layer1(8, 0)
+            layer1(8, 1)
+            quantize_x(10)
+            sign_w(2, 0, 1)
+            quantize_h(2)
+            interleave_w(2, 0, 1, vector_copy)
+            layer1(10, 0)
+            layer1(10, 1)
+            quantize_x(12)
+            quantize_w(2, 0, 0)
+            quantize_w(2, 0, 1)
+            layer1(12, 0)
+            layer1(12, 1)
+
+            quantize_h(4)
+            quantize_h(6)
+            for group in (0, 1, 2, 4):
+                layer2(group, 0)
+            relu_w(2, 1, 0)
+            quantize_x(13)
+            quantize_x(15)
+            layer1(13, 0)
+            layer1(13, 1)
+            quantize_h(8)
+            quantize_h(10)
+            sign_w(2, 1, 0)
+            relu_w(2, 1, 1)
+            quantize_h(12)
+            sign_w(2, 1, 1)
+            interleave_w(2, 1, 0, vector_copy)
+            interleave_w(2, 1, 1, vector_copy)
+            for group in (6, 8, 10, 12):
+                layer2(group, 0)
+            quantize_h(13)
+            layer2(13, 0)
+
+            quantize_w(2, 1, 0)
+            quantize_w(2, 1, 1)
+            odd_tiles = range(1, 12, 2)
+            for group in (0, 1, 2, 4, 6, 8, 10):
+                layer2(group, 1, odd_tiles)
+            layer1(15, 0)
+            layer1(15, 1)
+            quantize_h(15)
+            for group in (12, 13):
+                layer2(group, 1)
+            layer2(15, 0)
+            layer2(15, 1)

from contextlib import ExitStack

import concourse.mybir as mybir
from concourse.masks import make_identity

TOKENS, D, F, N = 2048, 1024, 1024, 1024
FLOPS = 2 * TOKENS * D * F + 2 * TOKENS * F * N

F32 = mybir.dt.float32
BF16 = mybir.dt.bfloat16
U32 = mybir.dt.uint32
U8 = mybir.dt.uint8
FP8 = mybir.dt.float8_e4m3fn
FP8X4 = mybir.dt.float8_e4m3fn_x4
MAX = mybir.AluOpType.max
MULT = mybir.AluOpType.mult
RELU = mybir.ActivationFunctionType.Relu

P = 128
PACK = 4
HALF = P * PACK

LOADS = ((0, 2), (2, 2), (4, 4), (8, 4), (12, 4))
GROUPS = ((0, 1), (1, 1), (2, 2), (4, 2), (6, 2), (8, 2), (10, 2), (12, 1), (13, 2), (15, 1))


def tile_sparse_connect_kernel(tc, x_bytes, x_scale, th1, sign1, th2, sign2, relu, out):
    assert relu == 1
    nc = tc.nc
    x_rows = x_bytes.flatten_outer_dims()
    out_rows = out.flatten_outer_dims()
    w1_hbm = [a.rearrange("(g p j) f -> g p j f", p=P, j=PACK) for a in (th1, sign1)]
    w2_hbm = [a.rearrange("(g p j) f -> g p j f", p=P, j=PACK) for a in (th2, sign2)]
    group_size = dict(GROUPS)

    with ExitStack() as ctx:
        keep = ctx.enter_context(tc.tile_pool(name="keep", bufs=1))
        stage = ctx.enter_context(tc.tile_pool(name="stage", bufs=4))
        work = ctx.enter_context(tc.tile_pool(name="work", bufs=6))
        psum = ctx.enter_context(tc.psum_pool(name="psum", bufs=8))

        identity = keep.tile([P, P], F32)
        make_identity(nc, identity[:])
        scale_column = keep.tile([P, 8], F32, align_bytes=64)
        scale = keep.tile([P, D], F32, align_bytes=64)
        x_codes_in = keep.tile([P, TOKENS // P, D], U8, align_bytes=64)

        theta, sign, grouped, w_codes, w_scales = {}, {}, {}, {}, {}
        x_tok, x_turned, x_grouped, x_codes, x_scales = {}, {}, {}, {}, {}
        h_grouped, h_codes, h_scales = {}, {}, {}

        def tiles_of(group):
            return range(group, group + group_size[group])


        def row_parts(layer, half, g):
            return (slice(0, 2), slice(2, 4)) if (layer, half, g) == (1, 0, 0) else (slice(0, 4),)

        def load_w1(half, g):
            cols = slice(half * HALF, (half + 1) * HALF)
            th = stage.tile([P, PACK, HALF], BF16, name="theta1", align_bytes=64)
            sg = stage.tile([P, PACK, HALF], BF16, name="sign1", align_bytes=64)
            for dst, src in ((th, w1_hbm[0][g]), (sg, w1_hbm[1][g])):
                for rows in row_parts(1, half, g):
                    nc.sync.dma_start(out=dst[:, rows], in_=src[:, rows, cols])
            theta[1, half, g], sign[1, half, g] = th[:], sg[:]

        def load_w2(g):
            th = stage.tile([P, PACK, N], BF16, name="theta2", bufs=2, align_bytes=64)
            nc.sync.dma_start(out=th[:], in_=w2_hbm[0][g])
            sg = stage.tile([P, PACK, N], BF16, name="sign2", bufs=2, align_bytes=64)
            nc.sync.dma_start(out=sg[:], in_=w2_hbm[1][g])
            for half in (0, 1):
                cols = slice(half * HALF, (half + 1) * HALF)
                theta[2, half, g], sign[2, half, g] = th[:, :, cols], sg[:, :, cols]

        def load_x(first, count):
            nc.sync.dma_start(
                out=x_codes_in[:, first : first + count],
                in_=x_rows[first * P : (first + count) * P, :].rearrange("(p c) d -> p c d", c=count),
            )

        def spread_scale():
            for b in (0, 1):
                bank = psum.tile([P, PACK, P], F32, name="scale_bank", tag="bank")
                for c in range(PACK):
                    column = scale_column[:, PACK * b + c : PACK * b + c + 1]
                    nc.tensor.matmul(
                        out=bank[:, c], lhsT=column.to_broadcast([P, P]), rhs=identity[:], start=True, stop=True
                    )
                nc.scalar.copy(
                    out=scale[:].rearrange("p (q c) -> p q c", c=8)[:, :, PACK * b : PACK * (b + 1)],
                    in_=bank[:].rearrange("p c q -> p q c"),
                )


        def relu_w(layer, half, g):
            th = theta[layer, half, g]
            for rows in row_parts(layer, half, g):
                nc.vector.tensor_scalar(out=th[:, rows], in0=th[:, rows], scalar1=0.0, scalar2=None, op0=MAX)

        def sign_w(layer, half, g):
            th, sg = theta[layer, half, g], sign[layer, half, g]
            for rows in row_parts(layer, half, g):
                nc.vector.tensor_tensor(out=th[:, rows], in0=th[:, rows], in1=sg[:, rows], op=MULT)

        def interleave_w(layer, half, g, copy):
            w = stage.tile([P, HALF * PACK], BF16, name="w_grouped", bufs=3, align_bytes=64)
            th = theta[layer, half, g]
            if layer == 1:
                copy(
                    out=w[:].rearrange("p (t m j) -> p m t j", t=PACK, j=PACK),
                    in_=th.rearrange("p j (m t) -> p m t j", t=PACK),
                )
            else:
                copy(
                    out=w[:].rearrange("p (c i j) -> p c j i", i=4, j=PACK),
                    in_=th.rearrange("p j (c i) -> p c j i", i=4),
                )
            grouped[layer, half, g] = w

        def quantize_w(layer, half, g):
            codes = keep.tile([P, HALF], U32, name=f"w_codes{layer}{half}{g}", align_bytes=64)
            scales = keep.tile([P, HALF], U8, name=f"w_scales{layer}{half}{g}", align_bytes=64)
            nc.vector.quantize_mx(out=codes[:].bitcast(FP8X4), scales=scales[:], in_=grouped[layer, half, g][:])
            w_codes[layer, half, g], w_scales[layer, half, g] = codes, scales


        def multiply_x(i):
            t = work.tile([P, D], BF16, name="x_tok", align_bytes=64)
            nc.vector.tensor_tensor(out=t[:], in0=x_codes_in[:, i].bitcast(FP8), in1=scale[:], op=MULT)
            x_tok[i] = t

        def turn_x(i):
            words = x_tok[i][:].bitcast(F32)
            bank = psum.tile([P, 2, 2, P], F32, name="x_bank", tag="bank")
            for g in (0, 1):
                for u in (0, 1):
                    nc.tensor.transpose(bank[:, g, u], words[:, 256 * g + u : 256 * (g + 1) : 2], identity[:])
            group = max(first for first, _ in GROUPS if first <= i)
            if i == group:
                x_grouped[group] = work.tile([P, group_size[group], 2, P, 2], F32, name="x_grouped", bufs=4, align_bytes=64)
            nc.scalar.copy(out=x_grouped[group][:, i - group], in_=bank[:].rearrange("p g u r -> p g r u"))

        def quantize_x(group):
            count = group_size[group]
            codes = work.tile([P, count, 2, P], U32, name="x_codes", bufs=6, align_bytes=64)
            scales = work.tile([P, count, 2, P], U8, name="x_scales", bufs=6, align_bytes=64)
            nc.vector.quantize_mx(
                out=codes[:].rearrange("p c g r -> p (c g r)").bitcast(FP8X4),
                scales=scales[:].rearrange("p c g r -> p (c g r)"),
                in_=x_grouped[group][:].rearrange("p c g r u -> p (c g r u)").bitcast(BF16),
            )
            for c, i in enumerate(tiles_of(group)):
                x_codes[i], x_scales[i] = codes[:, c], scales[:, c]


        def layer1(group, half):
            if half == 0:
                h_grouped[group] = work.tile(
                    [P, group_size[group], 2, P, PACK], BF16, name="h_grouped", bufs=7, align_bytes=64
                )
            for c, i in enumerate(tiles_of(group)):
                bank = psum.tile([P, PACK, P], F32, name="h_bank", tag="bank")
                for t in range(PACK):
                    cols = slice(t * P, (t + 1) * P)
                    for g in (0, 1):
                        nc.tensor.matmul_mx(
                            out=bank[:, t],
                            lhsT=w_codes[1, half, g][:, cols].bitcast(FP8X4),
                            lhsT_scale=w_scales[1, half, g][:, cols],
                            rhs=x_codes[i][:, g].bitcast(FP8X4),
                            rhs_scale=x_scales[i][:, g],
                            start=(g == 0),
                            stop=(g == 1),
                        )
                nc.scalar.activation(
                    out=h_grouped[group][:, c, half], in_=bank[:].rearrange("p t n -> p n t"), func=RELU
                )

        def quantize_h(group):
            count = group_size[group]
            codes = work.tile([P, count, 2, P], U32, name="h_codes", bufs=len(GROUPS), align_bytes=64)
            scales = work.tile([P, count, 2, P], U8, name="h_scales", bufs=len(GROUPS), align_bytes=64)
            nc.vector.quantize_mx(
                out=codes[:].rearrange("p c g n -> p (c g n)").bitcast(FP8X4),
                scales=scales[:].rearrange("p c g n -> p (c g n)"),
                in_=h_grouped[group][:].rearrange("p c g n t -> p (c g n t)"),
            )
            for c, i in enumerate(tiles_of(group)):
                h_codes[i], h_scales[i] = codes[:, c], scales[:, c]


        def layer2(group, half, vector_tiles=()):
            cols = slice(half * HALF, (half + 1) * HALF)
            for i in tiles_of(group):
                bank = psum.tile([P, HALF], F32, name="out_bank", tag="bank")
                for g in (0, 1):
                    nc.tensor.matmul_mx(
                        out=bank[:],
                        lhsT=h_codes[i][:, g].bitcast(FP8X4),
                        lhsT_scale=h_scales[i][:, g],
                        rhs=w_codes[2, half, g][:].bitcast(FP8X4),
                        rhs_scale=w_scales[2, half, g][:],
                        start=(g == 0),
                        stop=(g == 1),
                    )
                result = work.tile([P, HALF], F32, name="result", bufs=8, align_bytes=64)
                if i in vector_tiles:
                    nc.vector.tensor_scalar(out=result[:], in0=bank[:], scalar1=0.0, scalar2=None, op0=MAX)
                else:
                    nc.scalar.activation(out=result[:], in_=bank[:], func=RELU)
                first, count = max(load for load in LOADS if load[0] <= i)
                rows = out_rows[first * P : (first + count) * P, :].rearrange("(p c) n -> c p n", c=count)
                nc.sync.dma_start(out=rows[i - first][:, cols], in_=result[:])


        scalar_copy, vector_copy = nc.scalar.copy, nc.vector.tensor_copy

        with tc.manual_schedule():
            nc.scalar.dma_start(out=scale_column[:], in_=x_scale.rearrange("a b (p c) -> p (a b c)", c=8))
            load_w1(0, 0)
            load_x(*LOADS[0])
            load_w1(0, 1)
            load_x(*LOADS[1])
            load_w1(1, 0)
            load_w1(1, 1)
            load_x(*LOADS[2])
            load_w2(0)
            load_w2(1)
            load_x(*LOADS[3])
            load_x(*LOADS[4])
            spread_scale()

            relu_w(1, 0, 0)
            sign_w(1, 0, 0)
            interleave_w(1, 0, 0, scalar_copy)
            relu_w(1, 0, 1)
            multiply_x(0)
            turn_x(0)
            sign_w(1, 0, 1)
            interleave_w(1, 0, 1, scalar_copy)
            multiply_x(1)
            turn_x(1)
            relu_w(1, 1, 0)
            multiply_x(2)
            turn_x(2)
            quantize_x(0)
            sign_w(1, 1, 0)
            interleave_w(1, 1, 0, scalar_copy)
            relu_w(1, 1, 1)
            multiply_x(3)
            sign_w(1, 1, 1)
            interleave_w(1, 1, 1, scalar_copy)
            turn_x(3)
            multiply_x(4)
            turn_x(4)
            quantize_w(1, 0, 0)
            quantize_w(1, 0, 1)
            multiply_x(5)
            turn_x(5)
            layer1(0, 0)
            for i in (6, 7):
                multiply_x(i)
                turn_x(i)
            quantize_x(1)
            quantize_x(2)
            quantize_w(1, 1, 0)
            quantize_w(1, 1, 1)

            layer1(1, 0)
            layer1(2, 0)
            relu_w(2, 0, 0)
            quantize_x(4)
            layer1(0, 1)
            layer1(1, 1)
            sign_w(2, 0, 0)
            interleave_w(2, 0, 0, scalar_copy)
            layer1(2, 1)
            quantize_x(6)
            layer1(4, 0)
            layer1(4, 1)
            for i in range(8, 12):
                multiply_x(i)
                turn_x(i)
            layer1(6, 0)
            layer1(6, 1)
            for i in range(12, 16):
                multiply_x(i)
                turn_x(i)
            quantize_x(8)
            relu_w(2, 0, 1)
            quantize_h(0)
            quantize_h(1)
            layer1(8, 0)
            layer1(8, 1)
            quantize_x(10)
            sign_w(2, 0, 1)
            quantize_h(2)
            interleave_w(2, 0, 1, vector_copy)
            layer1(10, 0)
            layer1(10, 1)
            quantize_x(12)
            quantize_w(2, 0, 0)
            quantize_w(2, 0, 1)
            layer1(12, 0)
            layer1(12, 1)

            quantize_h(4)
            quantize_h(6)
            for group in (0, 1, 2, 4):
                layer2(group, 0)
            relu_w(2, 1, 0)
            quantize_x(13)
            quantize_x(15)
            layer1(13, 0)
            layer1(13, 1)
            quantize_h(8)
            quantize_h(10)
            sign_w(2, 1, 0)
            relu_w(2, 1, 1)
            quantize_h(12)
            sign_w(2, 1, 1)
            interleave_w(2, 1, 0, vector_copy)
            interleave_w(2, 1, 1, vector_copy)
            for group in (6, 8, 10, 12):
                layer2(group, 0)
            quantize_h(13)
            layer2(13, 0)

            quantize_w(2, 1, 0)
            quantize_w(2, 1, 1)
            odd_tiles = range(1, 12, 2)
            for group in (0, 1, 2, 4, 6, 8, 10):
                layer2(group, 1, odd_tiles)
            layer1(15, 0)
            layer1(15, 1)
            quantize_h(15)
            for group in (12, 13):
                layer2(group, 1)
            layer2(15, 0)
            layer2(15, 1)
